import numpy as np
import ml_dtypes


def mxq(x, axis, fmt="e4m3"):
    dtype, down = {"e4m3": (ml_dtypes.float8_e4m3fn, 7), "e5m2": (ml_dtypes.float8_e5m2, 14)}[fmt]
    v = np.moveaxis(np.asarray(x, np.float32).astype(ml_dtypes.bfloat16).astype(np.float64), axis, -1)
    blocks = v.reshape(v.shape[:-1] + (-1, 32))
    amax = np.abs(blocks).max(-1, keepdims=True)
    byte = np.maximum(np.where(amax > 0, np.frexp(amax)[1] - 1 + 127, 0) - down, 1)
    scale = np.exp2(byte - 127.0)
    codes = (blocks / scale).astype(np.float32).astype(dtype).astype(np.float64)
    return np.moveaxis((codes * scale).reshape(v.shape), -1, axis)


WIDE = False


def mx_kscale(k):
    if not WIDE:
        return np.ones(k)
    levels = np.array([18, -18])
    if k % 512:
        return np.exp2(np.random.permutation(np.resize(levels, k // 32))).repeat(32)
    a = np.empty((k // 512, 16))
    for p in range(k // 512):
        a[p, :8] = np.random.permutation(np.resize(levels, 8))
        for g in range(8):
            far = levels[np.abs(levels - a[p, g]) >= 10]
            a[p, g + 8] = far[np.random.randint(len(far))]
    return np.exp2(a.ravel()).repeat(32)


BF16 = ml_dtypes.bfloat16


def bf(x):
    return np.asarray(x, np.float32).astype(BF16)


def f64(x):
    return np.asarray(x).astype(np.float64)


B, L0, L1, L2, L3 = 1024, 1024, 512, 512, 512
DT = 1.0
TAU_J = 10.0
TAU_M = 20.0
KAPPA_J = 0.25
THRESH = 0.4
X_DECAY = 20.0
P_FIRE = 0.2


def current_and_membrane(e_gen2, e_disc2, e_gen1, e_disc3, j2, v2, Eg1, Ed2):
    total = (-(f64(e_gen2) + f64(e_disc2))
             + f64(e_gen1) @ f64(Eg1).T
             + f64(e_disc3) @ f64(Ed2).T)
    j = f64(j2) + (DT / TAU_J) * (-KAPPA_J * f64(j2) + total)
    v = f64(v2) + (DT / TAU_M) * (-f64(v2) + j)
    return j, v


def setup_inputs():
    s = mx_kscale(B)[:, None]
    u = mx_kscale(L2)
    e_gen2 = bf(np.random.random((B, L2)) * 2.0 + np.random.standard_normal((B, L2)) * 0.7)
    e_disc2 = bf(np.random.random((B, L2)) * 2.0 + np.random.standard_normal((B, L2)) * 0.7)
    e_gen1_0 = bf(np.random.random((B, L1)) * 2.0 + np.random.standard_normal((B, L1)) * 0.7)
    e_disc3 = bf((np.random.random((B, L3)) < P_FIRE) + np.random.standard_normal((B, L3)) * 0.7)
    j2 = bf(np.random.standard_normal((B, L2)) * 1.5)
    v2 = bf(np.random.standard_normal((B, L2)) * 0.4)
    x2 = bf(np.random.random((B, L2)) * 2.0)
    Eg1_0 = bf(np.random.standard_normal((L2, L1)) * 2.0 / np.sqrt(L1))
    Ed2 = bf(np.random.standard_normal((L2, L3)) * 2.0 / np.sqrt(L3))
    _, v = current_and_membrane(e_gen2, e_disc2, e_gen1_0, e_disc3, j2, v2, Eg1_0, Ed2)
    side = np.where(v > THRESH, 1.0, -1.0)
    v2 = bf(f64(v2) + np.where(np.abs(v - THRESH) < 0.02, 0.05 * side, 0.0))
    _, v = current_and_membrane(e_gen2, e_disc2, e_gen1_0, e_disc3, j2, v2, Eg1_0, Ed2)
    cols = np.repeat(np.array([1.0, 16.0, 1.0, 1.0]), L2)
    g = bf(np.random.standard_normal((B, 4 * L2)) * np.exp2(np.random.randint(-6, 1, (B, 1))) * 4.0 * cols
           / s * np.tile(u, 4))
    return {
        "e_gen2": e_gen2,
        "e_disc2": e_disc2,
        "e_gen1": bf(f64(e_gen1_0) * s),
        "e_disc3": e_disc3,
        "j2": j2,
        "v2": v2,
        "x2": x2,
        "Eg1": bf(f64(Eg1_0) / u[:, None]),
        "Ed2": Ed2,
        "v_pre": np.asarray(v, np.float32),
        "grad_out": g,
    }


def reference(e_gen2, e_disc2, e_gen1, e_disc3, j2, v2, x2, Eg1, Ed2, v_pre, grad_out):
    g = f64(grad_out)
    gj = g[:, :L2]
    gv = g[:, L2:2 * L2]
    keep = np.where(f64(v_pre) > THRESH, 0.0, 1.0)
    dz = (DT / TAU_J) * (gj + (DT / TAU_M) * keep * gv)
    dx = mxq(dz, 1, "e5m2") @ mxq(f64(Eg1), 0, "e4m3")
    dw = mxq(dz, 0, "e5m2").T @ mxq(f64(e_gen1), 0, "e4m3")
    return dx, dw

@@ -1,0 +1,267 @@
+from contextlib import ExitStack
+
+import concourse.mybir as mybir
+from concourse.masks import make_identity
+
+F32 = mybir.dt.float32
+BF16 = mybir.dt.bfloat16
+U32 = mybir.dt.uint32
+U8 = mybir.dt.uint8
+E4M3 = mybir.dt.float8_e4m3fn_x4
+E5M2 = mybir.dt.float8_e5m2_x4
+OP = mybir.AluOpType
+COPY = mybir.ActivationFunctionType.Copy
+
+P = 128
+PACK = 4
+N = 512
+TOKENS = 1024
+FLOPS = 2 * 2 * TOKENS * N * N
+BYTES = TOKENS * N * (4 + 2 + 2 + 2) + N * N * 2 + TOKENS * N * 4 + N * N * 4
+
+
+def tile_bspncn_pb_v_kernel(tc, e_gen2, e_disc2, e_gen1, e_disc3, j2, v2, x2, Eg1, Ed2, v_pre, grad_out, out_0, out_1):
+    nc = tc.nc
+    v_hbm = v_pre.rearrange("(g p j) w -> g p j w", p=P, j=PACK)
+    g_hbm = grad_out.rearrange("(g p j) w -> g p j w", p=P, j=PACK)
+    e_hbm = e_gen1.rearrange("(g p j) w -> g p j w", p=P, j=PACK)
+    eg_hbm = Eg1.rearrange("(p j) w -> p j w", j=PACK)
+    o0_hbm = out_0.rearrange("(g p j) w -> g p j w", p=P, j=PACK)
+
+    with ExitStack() as ctx:
+        keep = ctx.enter_context(tc.tile_pool(name="keep", bufs=1))
+        t_psum = ctx.enter_context(tc.psum_pool(name="t_psum", bufs=2))
+        o0_psum = ctx.enter_context(tc.psum_pool(name="o0_psum", bufs=2))
+        o1_psum = ctx.enter_context(tc.psum_pool(name="o1_psum", bufs=1))
+
+        def sb(name, shape, dtype):
+            return keep.tile(shape, dtype, name=name, align_bytes=64)
+
+        ident = sb("ident", [P, P], F32)
+        v_t = [sb(f"v{i}", [P, 2, N], F32) for i in range(4)]
+        g_t = [sb(f"g{i}", [P, 2, 2 * N], BF16) for i in range(4)]
+        e_raw = [sb(f"e{g}", [P, PACK, N], BF16) for g in range(2)]
+        eg_raw = sb("eg", [P, PACK, N], BF16)
+        m_t = [sb(f"m{k}", [P, N], BF16) for k in range(8)]
+        s_t = [sb(f"s{g}", [P, PACK, N], F32) for g in range(2)]
+        d_t = [sb(f"d{g}", [P, N, PACK], BF16) for g in range(2)]
+        e_t = [sb(f"ei{g}", [P, N, PACK], BF16) for g in range(2)]
+        eg_t = sb("egi", [P, N, PACK], BF16)
+        x_t = [sb(f"x{i}", [P, 2, P, PACK], BF16) for i in range(4)]
+        dc = [sb(f"dc{g}", [P, N], U32) for g in range(2)]
+        dsc = [sb(f"ds{g}", [P, N], U8) for g in range(2)]
+        ec = [sb(f"ec{g}", [P, N], U32) for g in range(2)]
+        esc = [sb(f"es{g}", [P, N], U8) for g in range(2)]
+        egc = sb("egc", [P, N], U32)
+        egs = sb("egs", [P, N], U8)
+        xc = [sb(f"xc{i}", [P, 2 * P], U32) for i in range(4)]
+        xs = [sb(f"xs{i}", [P, 2 * P], U8) for i in range(4)]
+        r0 = [sb(f"r0{i}", [P, 2, N], F32) for i in range(4)]
+        r1 = [sb(f"r1{t}", [P, N], F32) for t in range(4)]
+
+        def load_v(i, a, b):
+            nc.sync.dma_start(out=v_t[i][:, a:b, :], in_=v_hbm[i // 2][:, 2 * (i % 2) + a:2 * (i % 2) + b, :])
+
+        def load_g(i, a, b):
+            nc.sync.dma_start(out=g_t[i][:, a:b, :], in_=g_hbm[i // 2][:, 2 * (i % 2) + a:2 * (i % 2) + b, 0:2 * N])
+
+        def load_e(g):
+            nc.sync.dma_start(out=e_raw[g][:], in_=e_hbm[g])
+
+        def copy(eng, out, in_):
+            if eng == "V":
+                nc.vector.tensor_copy(out=out, in_=in_)
+            else:
+                nc.scalar.copy(out=out, in_=in_)
+
+        def four_by_four_in(ap):
+            return ap.rearrange("p j (c i) -> p c j i", i=4)
+
+        def four_by_four_out(ap):
+            return ap.rearrange("p (c i) j -> p c j i", i=4)
+
+        def inter(eng, dst, src, h):
+            c = slice(256 * h, 256 * h + 256)
+            copy(eng, four_by_four_out(dst[:, c, :]), four_by_four_in(src[:, :, c]))
+
+        def scale_round(eng, out, in_):
+            if eng == "V":
+                nc.vector.tensor_scalar(out=out, in0=in_, scalar1=0.1, scalar2=None, op0=OP.mult)
+            else:
+                nc.scalar.activation(out=out, in_=in_, func=COPY, scale=0.1)
+
+        def d_inter(eng, g, h):
+            c = slice(256 * h, 256 * h + 256)
+            scale_round(eng, four_by_four_out(d_t[g][:, c, :]), four_by_four_in(s_t[g][:, :, c]))
+
+        def quant(dst, sc, src, c0, w, fmt):
+            nc.vector.quantize_mx(out=dst[:, c0:c0 + w].bitcast(fmt), scales=sc[:, c0:c0 + w],
+                                  in_=src[:, c0:c0 + w, :].rearrange("p w j -> p (w j)"))
+
+        def op1(k):
+            i, jj = divmod(k, 2)
+            nc.vector.scalar_tensor_tensor(out=m_t[k][:], in0=v_t[i][:, jj, :], scalar=0.4,
+                                           in1=g_t[i][:, jj, N:2 * N], op0=OP.is_le, op1=OP.mult)
+
+        def op2(k):
+            i, jj = divmod(k, 2)
+            nc.vector.scalar_tensor_tensor(out=s_t[k // 4][:, k % 4, :], in0=m_t[k][:], scalar=0.05,
+                                           in1=g_t[i][:, jj, 0:N], op0=OP.mult, op1=OP.add)
+
+        tps = {}
+
+        def tr(k):
+            tp = t_psum.tile([P, PACK, P], F32, name="tp")
+            tps[k] = tp
+            for t in range(PACK):
+                nc.tensor.transpose(tp[:, t, :], s_t[k // 4][:, k % 4, t::PACK], ident[:])
+
+        def tcopy(eng, k):
+            scale_round(eng, x_t[k // 2][:, k % 2, :, :], tps[k][:].rearrange("q t p -> q p t"))
+
+        def tq(i):
+            nc.vector.quantize_mx(out=xc[i][:].bitcast(E5M2), scales=xs[i][:],
+                                  in_=x_t[i][:].rearrange("q j p t -> q (j p t)"))
+
+        o0s = {}
+
+        def mm0(k):
+            i, jj = divmod(k, 2)
+            op = o0_psum.tile([P, N], F32, name="o0p")
+            o0s[k] = op
+            c = slice(P * jj, P * jj + P)
+            nc.tensor.matmul_mx(out=op[:], lhsT=xc[i][:, c].bitcast(E5M2), lhsT_scale=xs[i][:, c],
+                                rhs=egc[:].bitcast(E4M3), rhs_scale=egs[:], start=True, stop=True)
+
+        def oc0(eng, k):
+            copy(eng, r0[k // 2][:, k % 2, :], o0s[k][:])
+
+        def st0(i):
+            nc.sync.dma_start(out=o0_hbm[i // 2][:, 2 * (i % 2):2 * (i % 2) + 2, :], in_=r0[i][:])
+
+        def st0_unit(k):
+            nc.sync.dma_start(out=o0_hbm[k // 4][:, k % 4, :], in_=r0[k // 2][:, k % 2, :])
+
+        o1 = [o1_psum.tile([P, N], F32, name=f"o1p{t}") for t in range(4)]
+
+        def mm1(g, t):
+            c = slice(P * t, P * t + P)
+            nc.tensor.matmul_mx(out=o1[t][:], lhsT=dc[g][:, c].bitcast(E5M2), lhsT_scale=dsc[g][:, c],
+                                rhs=ec[g][:].bitcast(E4M3), rhs_scale=esc[g][:], start=(g == 0), stop=(g == 1))
+
+        def oc1(eng, t):
+            copy(eng, r1[t][:], o1[t][:])
+
+        def st1(t):
+            nc.sync.dma_start(out=out_1[P * t:P * t + P, :], in_=r1[t][:])
+
+        make_identity(nc, ident[:])
+        with tc.manual_schedule():
+            load_g(0, 0, 1)
+            load_v(0, 0, 1)
+            load_g(0, 1, 2)
+            load_v(0, 1, 2)
+            load_e(0)
+
+            load_v(1, 0, 2)
+            load_g(1, 0, 2)
+            nc.sync.dma_start(out=eg_raw[:], in_=eg_hbm)
+
+            load_g(2, 0, 2)
+            load_v(2, 0, 2)
+            load_v(3, 0, 2)
+            load_g(3, 0, 2)
+            load_e(1)
+            op1(0)
+            op2(0)
+            op1(1)
+            op2(1)
+            tr(0)
+            tr(1)
+            inter("S", e_t[0], e_raw[0], 0)
+            tcopy("S", 0)
+            tcopy("S", 1)
+            quant(ec[0], esc[0], e_t[0], 0, 256, E4M3)
+            inter("S", e_t[0], e_raw[0], 1)
+            inter("S", eg_t, eg_raw, 0)
+            op1(2)
+            op1(3)
+            op2(2)
+            op2(3)
+            tr(2)
+            tr(3)
+            inter("V", eg_t, eg_raw, 1)
+            d_inter("S", 0, 0)
+            tq(0)
+            quant(egc, egs, eg_t, 0, N, E4M3)
+            quant(ec[0], esc[0], e_t[0], 256, 256, E4M3)
+            quant(dc[0], dsc[0], d_t[0], 0, 256, E5M2)
+            tcopy("S", 2)
+            tcopy("S", 3)
+            mm0(0)
+            mm0(1)
+            mm1(0, 0)
+            mm1(0, 1)
+            oc0("S", 0)
+            oc0("S", 1)
+            st0(0)
+            d_inter("S", 0, 1)
+            op1(4)
+            op1(5)
+            op2(4)
+            op2(5)
+            tr(4)
+            tr(5)
+            op1(6)
+            tcopy("S", 4)
+            tcopy("S", 5)
+            tq(1)
+            op1(7)
+            mm0(2)
+            mm0(3)
+            oc0("S", 2)
+            oc0("S", 3)
+            st0(1)
+            op2(6)
+            tr(6)
+            op2(7)
+            tq(2)
+            mm0(4)
+            mm0(5)
+            tr(7)
+            inter("S", e_t[1], e_raw[1], 0)
+            inter("V", e_t[1], e_raw[1], 1)
+            d_inter("V", 1, 0)
+            quant(ec[1], esc[1], e_t[1], 256, 256, E4M3)
+            quant(dc[1], dsc[1], d_t[1], 0, 256, E5M2)
+            quant(ec[1], esc[1], e_t[1], 0, 256, E4M3)
+            mm1(1, 0)
+            mm1(1, 1)
+            oc0("S", 4)
+            st0_unit(4)
+            oc0("S", 5)
+            st0_unit(5)
+            tcopy("S", 6)
+            d_inter("V", 1, 1)
+            quant(dc[0], dsc[0], d_t[0], 256, 256, E5M2)
+            quant(dc[1], dsc[1], d_t[1], 256, 256, E5M2)
+            mm1(0, 2)
+            mm1(1, 2)
+            mm1(0, 3)
+            mm1(1, 3)
+            tcopy("V", 7)
+            tq(3)
+            mm0(6)
+            mm0(7)
+            oc1("S", 0)
+            st1(0)
+            oc1("S", 1)
+            st1(1)
+            oc1("S", 2)
+            st1(2)
+            oc1("S", 3)
+            st1(3)
+            oc0("V", 6)
+            st0_unit(6)
+            oc0("V", 7)
+            st0_unit(7)

@@ -16,6 +16,7 @@ P = 128
 PACK = 4
 N = 512
 TOKENS = 1024
+UNITS = 8
 FLOPS = 2 * 2 * TOKENS * N * N
 BYTES = TOKENS * N * (4 + 2 + 2 + 2) + N * N * 2 + TOKENS * N * 4 + N * N * 4
 
@@ -25,8 +26,9 @@ def tile_bspncn_pb_v_kernel(tc, e_gen2, e_disc2, e_gen1, e_disc3, j2, v2, x2, Eg
     v_hbm = v_pre.rearrange("(g p j) w -> g p j w", p=P, j=PACK)
     g_hbm = grad_out.rearrange("(g p j) w -> g p j w", p=P, j=PACK)
     e_hbm = e_gen1.rearrange("(g p j) w -> g p j w", p=P, j=PACK)
-    eg_hbm = Eg1.rearrange("(p j) w -> p j w", j=PACK)
     o0_hbm = out_0.rearrange("(g p j) w -> g p j w", p=P, j=PACK)
+    o1_hbm = out_1.rearrange("(q t) w -> t q w", t=PACK)
+    w_hbm = {"eg": Eg1.rearrange("(p j) w -> p j w", j=PACK), "e0": e_hbm[0], "e1": e_hbm[1]}
 
     with ExitStack() as ctx:
         keep = ctx.enter_context(tc.tile_pool(name="keep", bufs=1))
@@ -38,35 +40,29 @@ def tile_bspncn_pb_v_kernel(tc, e_gen2, e_disc2, e_gen1, e_disc3, j2, v2, x2, Eg
             return keep.tile(shape, dtype, name=name, align_bytes=64)
 
         ident = sb("ident", [P, P], F32)
-        v_t = [sb(f"v{i}", [P, 2, N], F32) for i in range(4)]
-        g_t = [sb(f"g{i}", [P, 2, 2 * N], BF16) for i in range(4)]
-        e_raw = [sb(f"e{g}", [P, PACK, N], BF16) for g in range(2)]
-        eg_raw = sb("eg", [P, PACK, N], BF16)
-        m_t = [sb(f"m{k}", [P, N], BF16) for k in range(8)]
+        v_t = [sb(f"v{k}", [P, N], F32) for k in range(UNITS)]
+        g_t = [sb(f"g{k}", [P, 2 * N], BF16) for k in range(UNITS)]
+        m_t = [sb(f"m{k}", [P, N], BF16) for k in range(UNITS)]
         s_t = [sb(f"s{g}", [P, PACK, N], F32) for g in range(2)]
-        d_t = [sb(f"d{g}", [P, N, PACK], BF16) for g in range(2)]
-        e_t = [sb(f"ei{g}", [P, N, PACK], BF16) for g in range(2)]
-        eg_t = sb("egi", [P, N, PACK], BF16)
-        x_t = [sb(f"x{i}", [P, 2, P, PACK], BF16) for i in range(4)]
-        dc = [sb(f"dc{g}", [P, N], U32) for g in range(2)]
-        dsc = [sb(f"ds{g}", [P, N], U8) for g in range(2)]
-        ec = [sb(f"ec{g}", [P, N], U32) for g in range(2)]
-        esc = [sb(f"es{g}", [P, N], U8) for g in range(2)]
-        egc = sb("egc", [P, N], U32)
-        egs = sb("egs", [P, N], U8)
-        xc = [sb(f"xc{i}", [P, 2 * P], U32) for i in range(4)]
-        xs = [sb(f"xs{i}", [P, 2 * P], U8) for i in range(4)]
+        raw = {n: sb(f"raw_{n}", [P, PACK, N], BF16) for n in ("eg", "e0", "e1")}
+        names = ("eg", "e0", "e1", "d0", "d1")
+        grouped = {n: sb(f"grp_{n}", [P, N, PACK], BF16) for n in names}
+        codes = {n: sb(f"codes_{n}", [P, N], U32) for n in names}
+        scales = {n: sb(f"scales_{n}", [P, N], U8) for n in names}
+        x_t = [sb(f"x{k}", [P, P, PACK], BF16) for k in range(UNITS)]
+        xc = [sb(f"xc{k}", [P, P], U32) for k in range(UNITS)]
+        xs = [sb(f"xs{k}", [P, P], U8) for k in range(UNITS)]
         r0 = [sb(f"r0{i}", [P, 2, N], F32) for i in range(4)]
         r1 = [sb(f"r1{t}", [P, N], F32) for t in range(4)]
 
-        def load_v(i, a, b):
-            nc.sync.dma_start(out=v_t[i][:, a:b, :], in_=v_hbm[i // 2][:, 2 * (i % 2) + a:2 * (i % 2) + b, :])
+        def load_v(k, n=1):
+            nc.sync.dma_start(out=v_t[k][:], in_=v_hbm[k // 4][:, k % 4, :])
 
-        def load_g(i, a, b):
-            nc.sync.dma_start(out=g_t[i][:, a:b, :], in_=g_hbm[i // 2][:, 2 * (i % 2) + a:2 * (i % 2) + b, 0:2 * N])
+        def load_g(k, n=1):
+            nc.sync.dma_start(out=g_t[k][:], in_=g_hbm[k // 4][:, k % 4, 0:2 * N])
 
-        def load_e(g):
-            nc.sync.dma_start(out=e_raw[g][:], in_=e_hbm[g])
+        def load_w(name):
+            nc.sync.dma_start(out=raw[name][:], in_=w_hbm[name])
 
         def copy(eng, out, in_):
             if eng == "V":
@@ -74,39 +70,40 @@ def tile_bspncn_pb_v_kernel(tc, e_gen2, e_disc2, e_gen1, e_disc3, j2, v2, x2, Eg
             else:
                 nc.scalar.copy(out=out, in_=in_)
 
-        def four_by_four_in(ap):
-            return ap.rearrange("p j (c i) -> p c j i", i=4)
-
-        def four_by_four_out(ap):
-            return ap.rearrange("p (c i) j -> p c j i", i=4)
-
-        def inter(eng, dst, src, h):
-            c = slice(256 * h, 256 * h + 256)
-            copy(eng, four_by_four_out(dst[:, c, :]), four_by_four_in(src[:, :, c]))
-
         def scale_round(eng, out, in_):
             if eng == "V":
                 nc.vector.tensor_scalar(out=out, in0=in_, scalar1=0.1, scalar2=None, op0=OP.mult)
             else:
                 nc.scalar.activation(out=out, in_=in_, func=COPY, scale=0.1)
 
-        def d_inter(eng, g, h):
-            c = slice(256 * h, 256 * h + 256)
-            scale_round(eng, four_by_four_out(d_t[g][:, c, :]), four_by_four_in(s_t[g][:, :, c]))
+        def four_by_four_in(ap):
+            return ap.rearrange("p j (c i) -> p c j i", i=4)
 
-        def quant(dst, sc, src, c0, w, fmt):
-            nc.vector.quantize_mx(out=dst[:, c0:c0 + w].bitcast(fmt), scales=sc[:, c0:c0 + w],
-                                  in_=src[:, c0:c0 + w, :].rearrange("p w j -> p (w j)"))
+        def four_by_four_out(ap):
+            return ap.rearrange("p (c i) j -> p c j i", i=4)
 
-        def op1(k):
-            i, jj = divmod(k, 2)
-            nc.vector.scalar_tensor_tensor(out=m_t[k][:], in0=v_t[i][:, jj, :], scalar=0.4,
-                                           in1=g_t[i][:, jj, N:2 * N], op0=OP.is_le, op1=OP.mult)
+        def inter(eng, name, c0, w):
+            copy(eng, four_by_four_out(grouped[name][:, c0:c0 + w, :]), four_by_four_in(raw[name][:, :, c0:c0 + w]))
 
-        def op2(k):
-            i, jj = divmod(k, 2)
-            nc.vector.scalar_tensor_tensor(out=s_t[k // 4][:, k % 4, :], in0=m_t[k][:], scalar=0.05,
-                                           in1=g_t[i][:, jj, 0:N], op0=OP.mult, op1=OP.add)
+        def d_inter(eng, g, c0, w):
+            scale_round(eng, four_by_four_out(grouped[f"d{g}"][:, c0:c0 + w, :]), four_by_four_in(s_t[g][:, :, c0:c0 + w]))
+
+        def quant(name, c0, w):
+            fmt = E5M2 if name[0] == "d" else E4M3
+            nc.vector.quantize_mx(out=codes[name][:, c0:c0 + w].bitcast(fmt), scales=scales[name][:, c0:c0 + w],
+                                  in_=grouped[name][:, c0:c0 + w, :].rearrange("p w j -> p (w j)"))
+
+        def mask(k, c0=0, w=N):
+            nc.vector.scalar_tensor_tensor(out=m_t[k][:, c0:c0 + w], in0=v_t[k][:, c0:c0 + w], scalar=0.4,
+                                           in1=g_t[k][:, N + c0:N + c0 + w], op0=OP.is_lt, op1=OP.mult)
+
+        def by_slot(ap):
+            return ap.rearrange("p (q t) -> p t q", t=PACK)
+
+        def summ(k, c0=0, w=N):
+            out = s_t[k // 4][:, k % 4, :].rearrange("p (t q) -> p t q", t=PACK)[:, :, c0 // PACK:(c0 + w) // PACK]
+            nc.vector.scalar_tensor_tensor(out=out, in0=by_slot(m_t[k][:, c0:c0 + w]), scalar=0.05,
+                                           in1=by_slot(g_t[k][:, c0:c0 + w]), op0=OP.mult, op1=OP.add)
 
         tps = {}
 
@@ -114,154 +111,163 @@ def tile_bspncn_pb_v_kernel(tc, e_gen2, e_disc2, e_gen1, e_disc3, j2, v2, x2, Eg
             tp = t_psum.tile([P, PACK, P], F32, name="tp")
             tps[k] = tp
             for t in range(PACK):
-                nc.tensor.transpose(tp[:, t, :], s_t[k // 4][:, k % 4, t::PACK], ident[:])
+                nc.tensor.transpose(tp[:, t, :], s_t[k // 4][:, k % 4, P * t:P * t + P], ident[:])
 
         def tcopy(eng, k):
-            scale_round(eng, x_t[k // 2][:, k % 2, :, :], tps[k][:].rearrange("q t p -> q p t"))
+            scale_round(eng, x_t[k][:], tps[k][:].rearrange("q t p -> q p t"))
 
-        def tq(i):
-            nc.vector.quantize_mx(out=xc[i][:].bitcast(E5M2), scales=xs[i][:],
-                                  in_=x_t[i][:].rearrange("q j p t -> q (j p t)"))
+        def tq(k):
+            nc.vector.quantize_mx(out=xc[k][:].bitcast(E5M2), scales=xs[k][:], in_=x_t[k][:].rearrange("q p t -> q (p t)"))
 
         o0s = {}
 
         def mm0(k):
-            i, jj = divmod(k, 2)
             op = o0_psum.tile([P, N], F32, name="o0p")
             o0s[k] = op
-            c = slice(P * jj, P * jj + P)
-            nc.tensor.matmul_mx(out=op[:], lhsT=xc[i][:, c].bitcast(E5M2), lhsT_scale=xs[i][:, c],
-                                rhs=egc[:].bitcast(E4M3), rhs_scale=egs[:], start=True, stop=True)
+            nc.tensor.matmul_mx(out=op[:], lhsT=xc[k][:].bitcast(E5M2), lhsT_scale=xs[k][:],
+                                rhs=codes["eg"][:].bitcast(E4M3), rhs_scale=scales["eg"][:], start=True, stop=True)
 
         def oc0(eng, k):
             copy(eng, r0[k // 2][:, k % 2, :], o0s[k][:])
 
-        def st0(i):
-            nc.sync.dma_start(out=o0_hbm[i // 2][:, 2 * (i % 2):2 * (i % 2) + 2, :], in_=r0[i][:])
-
-        def st0_unit(k):
-            nc.sync.dma_start(out=o0_hbm[k // 4][:, k % 4, :], in_=r0[k // 2][:, k % 2, :])
+        def st0(k, n=1):
+            nc.sync.dma_start(out=o0_hbm[k // 4][:, k % 4:k % 4 + n, :], in_=r0[k // 2][:, k % 2:k % 2 + n, :])
 
         o1 = [o1_psum.tile([P, N], F32, name=f"o1p{t}") for t in range(4)]
 
         def mm1(g, t):
             c = slice(P * t, P * t + P)
-            nc.tensor.matmul_mx(out=o1[t][:], lhsT=dc[g][:, c].bitcast(E5M2), lhsT_scale=dsc[g][:, c],
-                                rhs=ec[g][:].bitcast(E4M3), rhs_scale=esc[g][:], start=(g == 0), stop=(g == 1))
+            nc.tensor.matmul_mx(out=o1[t][:], lhsT=codes[f"d{g}"][:, c].bitcast(E5M2), lhsT_scale=scales[f"d{g}"][:, c],
+                                rhs=codes[f"e{g}"][:].bitcast(E4M3), rhs_scale=scales[f"e{g}"][:], start=(g == 0), stop=(g == 1))
 
         def oc1(eng, t):
             copy(eng, r1[t][:], o1[t][:])
 
         def st1(t):
-            nc.sync.dma_start(out=out_1[P * t:P * t + P, :], in_=r1[t][:])
+            nc.sync.dma_start(out=o1_hbm[t], in_=r1[t][:])
 
         make_identity(nc, ident[:])
         with tc.manual_schedule():
-            load_g(0, 0, 1)
-            load_v(0, 0, 1)
-            load_g(0, 1, 2)
-            load_v(0, 1, 2)
-            load_e(0)
-
-            load_v(1, 0, 2)
-            load_g(1, 0, 2)
-            nc.sync.dma_start(out=eg_raw[:], in_=eg_hbm)
-
-            load_g(2, 0, 2)
-            load_v(2, 0, 2)
-            load_v(3, 0, 2)
-            load_g(3, 0, 2)
-            load_e(1)
-            op1(0)
-            op2(0)
-            op1(1)
-            op2(1)
+            load_g(0,1)
+            load_v(0,1)
+            load_g(1,1)
+            load_v(1,1)
+            load_w("eg")
+            load_g(2,1)
+            load_v(2,1)
+            load_w("e0")
+            for k in range(3,6):
+                load_g(k,1)
+                load_v(k,1)
+            load_w("e1")
+            for k in range(6,8):
+                load_g(k,1)
+                load_v(k,1)
+            mask(0,0,256)
+            mask(0,256,256)
+            summ(0,0,256)
+            summ(0,256,256)
             tr(0)
+            mask(1,0,256)
+            mask(1,256,256)
+            summ(1,0,256)
+            summ(1,256,256)
             tr(1)
-            inter("S", e_t[0], e_raw[0], 0)
-            tcopy("S", 0)
-            tcopy("S", 1)
-            quant(ec[0], esc[0], e_t[0], 0, 256, E4M3)
-            inter("S", e_t[0], e_raw[0], 1)
-            inter("S", eg_t, eg_raw, 0)
-            op1(2)
-            op1(3)
-            op2(2)
-            op2(3)
+            inter("S","eg",0,256)
+            inter("V","eg",256,256)
+            tcopy("S",0)
+            tcopy("S",1)
+            mask(2)
+            quant("eg",256,256)
+            summ(2)
             tr(2)
-            tr(3)
-            inter("V", eg_t, eg_raw, 1)
-            d_inter("S", 0, 0)
+            quant("eg",0,256)
+            inter("S","e0",0,256)
+            inter("V","e0",256,256)
             tq(0)
-            quant(egc, egs, eg_t, 0, N, E4M3)
-            quant(ec[0], esc[0], e_t[0], 256, 256, E4M3)
-            quant(dc[0], dsc[0], d_t[0], 0, 256, E5M2)
-            tcopy("S", 2)
-            tcopy("S", 3)
             mm0(0)
-            mm0(1)
-            mm1(0, 0)
-            mm1(0, 1)
-            oc0("S", 0)
-            oc0("S", 1)
-            st0(0)
-            d_inter("S", 0, 1)
-            op1(4)
-            op1(5)
-            op2(4)
-            op2(5)
-            tr(4)
-            tr(5)
-            op1(6)
-            tcopy("S", 4)
-            tcopy("S", 5)
             tq(1)
-            op1(7)
-            mm0(2)
-            mm0(3)
-            oc0("S", 2)
-            oc0("S", 3)
+            mm0(1)
+            tcopy("S",2)
+            oc0("S",0)
+            st0(0)
+            oc0("S",1)
             st0(1)
-            op2(6)
-            tr(6)
-            op2(7)
+            mask(3)
+            quant("e0",256,256)
+            summ(3)
+            tr(3)
+            d_inter("S",0,0,256)
+            tcopy("S",3)
+            mask(4)
             tq(2)
-            mm0(4)
-            mm0(5)
-            tr(7)
-            inter("S", e_t[1], e_raw[1], 0)
-            inter("V", e_t[1], e_raw[1], 1)
-            d_inter("V", 1, 0)
-            quant(ec[1], esc[1], e_t[1], 256, 256, E4M3)
-            quant(dc[1], dsc[1], d_t[1], 0, 256, E5M2)
-            quant(ec[1], esc[1], e_t[1], 0, 256, E4M3)
-            mm1(1, 0)
-            mm1(1, 1)
-            oc0("S", 4)
-            st0_unit(4)
-            oc0("S", 5)
-            st0_unit(5)
-            tcopy("S", 6)
-            d_inter("V", 1, 1)
-            quant(dc[0], dsc[0], d_t[0], 256, 256, E5M2)
-            quant(dc[1], dsc[1], d_t[1], 256, 256, E5M2)
-            mm1(0, 2)
-            mm1(1, 2)
-            mm1(0, 3)
-            mm1(1, 3)
-            tcopy("V", 7)
+            mm0(2)
+            summ(4)
+            tr(4)
+            oc0("S",2)
+            st0(2)
+            tcopy("S",4)
+            mask(5)
+            quant("e0",0,256)
+            summ(5)
+            tr(5)
             tq(3)
+            mm0(3)
+            d_inter("S",0,256,256)
+            oc0("S",3)
+            st0(3)
+            tcopy("S",5)
+            inter("V","e1",256,256)
+            tq(4)
+            mm0(4)
+            mask(6)
+            quant("d0",0,256)
+            summ(6)
+            tr(6)
+            mm1(0,0)
+            mm1(0,1)
+            oc0("S",4)
+            st0(4)
+            tcopy("S",6)
+            inter("V","e1",0,256)
+            tq(5)
+            mm0(5)
+            oc0("S",5)
+            st0(5)
+            mask(7)
+            quant("e1",256,256)
+            summ(7)
+            tr(7)
+            quant("e1",0,256)
+            tcopy("S",7)
+            d_inter("V",1,0,128)
+            tq(6)
             mm0(6)
-            mm0(7)
-            oc1("S", 0)
+            d_inter("V",1,128,128)
+            quant("d1",0,128)
+            mm1(1,0)
+            oc0("S",6)
+            st0(6)
+            quant("d0",256,256)
+            quant("d1",128,128)
+            mm1(1,1)
+            mm1(0,2)
+            mm1(0,3)
+            oc1("S",0)
             st1(0)
-            oc1("S", 1)
+            d_inter("V",1,256,128)
+            tq(7)
+            mm0(7)
+            d_inter("V",1,384,128)
+            quant("d1",256,128)
+            mm1(1,2)
+            oc1("S",1)
             st1(1)
-            oc1("S", 2)
+            quant("d1",384,128)
+            mm1(1,3)
+            oc0("S",7)
+            st0(7)
+            oc1("V",2)
             st1(2)
-            oc1("S", 3)
+            oc1("S",3)
             st1(3)
-            oc0("V", 6)
-            st0_unit(6)
-            oc0("V", 7)
-            st0_unit(7)

@@ -19,6 +19,7 @@ TOKENS = 1024
 UNITS = 8
 FLOPS = 2 * 2 * TOKENS * N * N
 BYTES = TOKENS * N * (4 + 2 + 2 + 2) + N * N * 2 + TOKENS * N * 4 + N * N * 4
+VUNITS = (0, 1, 2, 3)
 
 
 def tile_bspncn_pb_v_kernel(tc, e_gen2, e_disc2, e_gen1, e_disc3, j2, v2, x2, Eg1, Ed2, v_pre, grad_out, out_0, out_1):
@@ -27,38 +28,40 @@ def tile_bspncn_pb_v_kernel(tc, e_gen2, e_disc2, e_gen1, e_disc3, j2, v2, x2, Eg
     g_hbm = grad_out.rearrange("(g p j) w -> g p j w", p=P, j=PACK)
     e_hbm = e_gen1.rearrange("(g p j) w -> g p j w", p=P, j=PACK)
     o0_hbm = out_0.rearrange("(g p j) w -> g p j w", p=P, j=PACK)
-    o1_hbm = out_1.rearrange("(q t) w -> t q w", t=PACK)
+    o1_hbm = out_1.rearrange("(q t) w -> q t w", t=PACK)
     w_hbm = {"eg": Eg1.rearrange("(p j) w -> p j w", j=PACK), "e0": e_hbm[0], "e1": e_hbm[1]}
 
     with ExitStack() as ctx:
         keep = ctx.enter_context(tc.tile_pool(name="keep", bufs=1))
         t_psum = ctx.enter_context(tc.psum_pool(name="t_psum", bufs=2))
-        o0_psum = ctx.enter_context(tc.psum_pool(name="o0_psum", bufs=2))
-        o1_psum = ctx.enter_context(tc.psum_pool(name="o1_psum", bufs=1))
+        b_psum = ctx.enter_context(tc.psum_pool(name="b_psum", bufs=1))
+        o_psum = ctx.enter_context(tc.psum_pool(name="o_psum", bufs=4))
 
         def sb(name, shape, dtype):
             return keep.tile(shape, dtype, name=name, align_bytes=64)
 
         ident = sb("ident", [P, P], F32)
-        v_t = [sb(f"v{k}", [P, N], F32) for k in range(UNITS)]
+        ident20 = sb("ident20", [P, P], BF16)
+        v_t = [sb(f"v{i}", [P, 2, N], F32) for i in range(UNITS // 2)]
         g_t = [sb(f"g{k}", [P, 2 * N], BF16) for k in range(UNITS)]
-        m_t = [sb(f"m{k}", [P, N], BF16) for k in range(UNITS)]
-        s_t = [sb(f"s{g}", [P, PACK, N], F32) for g in range(2)]
+        m_t = {k: sb(f"m{k}", [P, N], BF16) for k in VUNITS}
+        s_all = sb("s_all", [P, PACK, N], F32)
+        s_t = [s_all[:, j, :] for j in range(PACK)] + [sb(f"s{k}", [P, N], F32)[:] for k in range(PACK)]
         raw = {n: sb(f"raw_{n}", [P, PACK, N], BF16) for n in ("eg", "e0", "e1")}
         names = ("eg", "e0", "e1", "d0", "d1")
         grouped = {n: sb(f"grp_{n}", [P, N, PACK], BF16) for n in names}
         codes = {n: sb(f"codes_{n}", [P, N], U32) for n in names}
         scales = {n: sb(f"scales_{n}", [P, N], U8) for n in names}
-        x_t = [sb(f"x{k}", [P, P, PACK], BF16) for k in range(UNITS)]
+        x_t = [sb(f"x{k}", [P, P * PACK], BF16) for k in range(UNITS)]
         xc = [sb(f"xc{k}", [P, P], U32) for k in range(UNITS)]
         xs = [sb(f"xs{k}", [P, P], U8) for k in range(UNITS)]
         r0 = [sb(f"r0{i}", [P, 2, N], F32) for i in range(4)]
-        r1 = [sb(f"r1{t}", [P, N], F32) for t in range(4)]
+        r1 = [sb(f"r1{i}", [P, 2, N], F32) for i in range(2)]
 
-        def load_v(k, n=1):
-            nc.sync.dma_start(out=v_t[k][:], in_=v_hbm[k // 4][:, k % 4, :])
+        def load_v(k, n):
+            nc.sync.dma_start(out=v_t[k // 2][:, k % 2:k % 2 + n, :], in_=v_hbm[k // 4][:, k % 4:k % 4 + n, :])
 
-        def load_g(k, n=1):
+        def load_g(k):
             nc.sync.dma_start(out=g_t[k][:], in_=g_hbm[k // 4][:, k % 4, 0:2 * N])
 
         def load_w(name):
@@ -70,12 +73,6 @@ def tile_bspncn_pb_v_kernel(tc, e_gen2, e_disc2, e_gen1, e_disc3, j2, v2, x2, Eg
             else:
                 nc.scalar.copy(out=out, in_=in_)
 
-        def scale_round(eng, out, in_):
-            if eng == "V":
-                nc.vector.tensor_scalar(out=out, in0=in_, scalar1=0.1, scalar2=None, op0=OP.mult)
-            else:
-                nc.scalar.activation(out=out, in_=in_, func=COPY, scale=0.1)
-
         def four_by_four_in(ap):
             return ap.rearrange("p j (c i) -> p c j i", i=4)
 
@@ -86,43 +83,83 @@ def tile_bspncn_pb_v_kernel(tc, e_gen2, e_disc2, e_gen1, e_disc3, j2, v2, x2, Eg
             copy(eng, four_by_four_out(grouped[name][:, c0:c0 + w, :]), four_by_four_in(raw[name][:, :, c0:c0 + w]))
 
         def d_inter(eng, g, c0, w):
-            scale_round(eng, four_by_four_out(grouped[f"d{g}"][:, c0:c0 + w, :]), four_by_four_in(s_t[g][:, :, c0:c0 + w]))
+            out = four_by_four_out(grouped[f"d{g}"][:, c0:c0 + w, :])
+            in_ = four_by_four_in(s_all[:, :, c0:c0 + w])
+            if eng == "V":
+                nc.vector.tensor_scalar(out=out, in0=in_, scalar1=0.005, scalar2=None, op0=OP.mult)
+            else:
+                nc.scalar.activation(out=out, in_=in_, func=COPY, scale=0.005)
 
         def quant(name, c0, w):
             fmt = E5M2 if name[0] == "d" else E4M3
             nc.vector.quantize_mx(out=codes[name][:, c0:c0 + w].bitcast(fmt), scales=scales[name][:, c0:c0 + w],
                                   in_=grouped[name][:, c0:c0 + w, :].rearrange("p w j -> p (w j)"))
 
-        def mask(k, c0=0, w=N):
-            nc.vector.scalar_tensor_tensor(out=m_t[k][:, c0:c0 + w], in0=v_t[k][:, c0:c0 + w], scalar=0.4,
-                                           in1=g_t[k][:, N + c0:N + c0 + w], op0=OP.is_lt, op1=OP.mult)
-
         def by_slot(ap):
             return ap.rearrange("p (q t) -> p t q", t=PACK)
 
-        def summ(k, c0=0, w=N):
-            out = s_t[k // 4][:, k % 4, :].rearrange("p (t q) -> p t q", t=PACK)[:, :, c0 // PACK:(c0 + w) // PACK]
-            nc.vector.scalar_tensor_tensor(out=out, in0=by_slot(m_t[k][:, c0:c0 + w]), scalar=0.05,
-                                           in1=by_slot(g_t[k][:, c0:c0 + w]), op0=OP.mult, op1=OP.add)
+        def mask(k):
+            v = v_t[k // 2][:, k % 2, :]
+            gv = g_t[k][:, N:2 * N]
+            if k in VUNITS:
+                nc.vector.scalar_tensor_tensor(out=m_t[k][:], in0=v, scalar=0.4, in1=gv, op0=OP.is_lt, op1=OP.mult)
+            else:
+                nc.vector.scalar_tensor_tensor(out=s_t[k].rearrange("p (t q) -> p q t", t=PACK),
+                                               in0=v.rearrange("p (q t) -> p q t", t=PACK), scalar=0.4,
+                                               in1=gv.rearrange("p (q t) -> p q t", t=PACK), op0=OP.is_lt, op1=OP.mult)
+
+        def summ(k):
+            nc.vector.scalar_tensor_tensor(out=s_t[k].rearrange("p (t q) -> p t q", t=PACK), in0=by_slot(g_t[k][:, 0:N]),
+                                           scalar=20.0, in1=by_slot(m_t[k][:]), op0=OP.mult, op1=OP.add)
 
         tps = {}
 
-        def tr(k):
+        def fwd(k):
             tp = t_psum.tile([P, PACK, P], F32, name="tp")
             tps[k] = tp
             for t in range(PACK):
-                nc.tensor.transpose(tp[:, t, :], s_t[k // 4][:, k % 4, P * t:P * t + P], ident[:])
+                nc.tensor.transpose(tp[:, t, :], s_t[k][:, P * t:P * t + P], ident[:])
+
+        def fmm(k):
+            tp = t_psum.tile([P, PACK, P], F32, name="tp")
+            tps[k] = tp
+            for t in range(PACK):
+                nc.tensor.matmul(tp[:, t, :], lhsT=g_t[k][:, t:N:PACK], rhs=ident20[:], start=(t == 0), stop=False)
+
+        def ftr(k):
+            for t in range(PACK):
+                nc.tensor.matmul(tps[k][:, t, :], lhsT=s_t[k][:, P * t:P * t + P], rhs=ident[:], is_transpose=True,
+                                 start=False, stop=(t == PACK - 1))
 
         def tcopy(eng, k):
-            scale_round(eng, x_t[k][:], tps[k][:].rearrange("q t p -> q p t"))
+            out = x_t[k][:].rearrange("q (p t) -> q p t", t=PACK)
+            in_ = tps[k][:].rearrange("q t p -> q p t")
+            if eng == "V":
+                nc.vector.tensor_scalar(out=out, in0=in_, scalar1=0.005, scalar2=None, op0=OP.mult)
+            else:
+                nc.scalar.activation(out=out, in_=in_, func=COPY, scale=0.005)
 
         def tq(k):
-            nc.vector.quantize_mx(out=xc[k][:].bitcast(E5M2), scales=xs[k][:], in_=x_t[k][:].rearrange("q p t -> q (p t)"))
+            nc.vector.quantize_mx(out=xc[k][:].bitcast(E5M2), scales=xs[k][:], in_=x_t[k][:])
+
+        bps = {}
+
+        def back(k):
+            if k % PACK == 0:
+                for u in range(2):
+                    bps[k // PACK, u] = b_psum.tile([P, PACK, P], F32, name=f"bp{u}")
+            words = x_t[k][:].bitcast(F32)
+            for u in range(2):
+                nc.tensor.transpose(bps[k // PACK, u][:, k % PACK, :], words[:, u:2 * P:2], ident[:])
+
+        def bcopy(eng, g, t):
+            halves = bps[g, t // 2][:].rearrange("p j q -> p (j q)").bitcast(BF16).rearrange("p (j q e) -> p e q j", j=PACK, e=2)
+            copy(eng, grouped[f"d{g}"][:, P * t:P * t + P, :], halves[:, t % 2, :, :])
 
         o0s = {}
 
         def mm0(k):
-            op = o0_psum.tile([P, N], F32, name="o0p")
+            op = o_psum.tile([P, N], F32, name="op")
             o0s[k] = op
             nc.tensor.matmul_mx(out=op[:], lhsT=xc[k][:].bitcast(E5M2), lhsT_scale=xs[k][:],
                                 rhs=codes["eg"][:].bitcast(E4M3), rhs_scale=scales["eg"][:], start=True, stop=True)
@@ -130,144 +167,123 @@ def tile_bspncn_pb_v_kernel(tc, e_gen2, e_disc2, e_gen1, e_disc3, j2, v2, x2, Eg
         def oc0(eng, k):
             copy(eng, r0[k // 2][:, k % 2, :], o0s[k][:])
 
-        def st0(k, n=1):
+        def st0(k, n):
             nc.sync.dma_start(out=o0_hbm[k // 4][:, k % 4:k % 4 + n, :], in_=r0[k // 2][:, k % 2:k % 2 + n, :])
 
-        o1 = [o1_psum.tile([P, N], F32, name=f"o1p{t}") for t in range(4)]
+        o1s = {}
 
-        def mm1(g, t):
+        def mm1(t):
+            op = o_psum.tile([P, N], F32, name="op")
+            o1s[t] = op
             c = slice(P * t, P * t + P)
-            nc.tensor.matmul_mx(out=o1[t][:], lhsT=codes[f"d{g}"][:, c].bitcast(E5M2), lhsT_scale=scales[f"d{g}"][:, c],
-                                rhs=codes[f"e{g}"][:].bitcast(E4M3), rhs_scale=scales[f"e{g}"][:], start=(g == 0), stop=(g == 1))
+            for g in range(2):
+                nc.tensor.matmul_mx(out=op[:], lhsT=codes[f"d{g}"][:, c].bitcast(E5M2), lhsT_scale=scales[f"d{g}"][:, c],
+                                    rhs=codes[f"e{g}"][:].bitcast(E4M3), rhs_scale=scales[f"e{g}"][:], start=(g == 0), stop=(g == 1))
 
         def oc1(eng, t):
-            copy(eng, r1[t][:], o1[t][:])
+            copy(eng, r1[t // 2][:, t % 2, :], o1s[t][:])
 
-        def st1(t):
-            nc.sync.dma_start(out=o1_hbm[t], in_=r1[t][:])
+        def st1(t, n):
+            nc.sync.dma_start(out=o1_hbm[:, t:t + n, :], in_=r1[t // 2][:, t % 2:t % 2 + n, :])
 
         make_identity(nc, ident[:])
         with tc.manual_schedule():
-            load_g(0,1)
-            load_v(0,1)
-            load_g(1,1)
-            load_v(1,1)
             load_w("eg")
-            load_g(2,1)
-            load_v(2,1)
+            load_g(0)
+            load_v(0, 1)
             load_w("e0")
-            for k in range(3,6):
-                load_g(k,1)
-                load_v(k,1)
+            for k in range(1, UNITS):
+                load_g(k)
+                load_v(k, 1)
             load_w("e1")
-            for k in range(6,8):
-                load_g(k,1)
-                load_v(k,1)
-            mask(0,0,256)
-            mask(0,256,256)
-            summ(0,0,256)
-            summ(0,256,256)
-            tr(0)
-            mask(1,0,256)
-            mask(1,256,256)
-            summ(1,0,256)
-            summ(1,256,256)
-            tr(1)
-            inter("S","eg",0,256)
-            inter("V","eg",256,256)
-            tcopy("S",0)
-            tcopy("S",1)
+            nc.scalar.activation(out=ident20[:], in_=ident[:], func=COPY, scale=20.0)
+            inter("S", "eg", 256, 256)
+            inter("V", "eg", 0, 256)
+            mask(0)
+            quant("eg", 0, 512)
+            summ(0)
+            fwd(0)
+            inter("S", "e0", 0, 512)
+            tcopy("S", 0)
+            mask(1)
+            summ(1)
+            fwd(1)
             mask(2)
-            quant("eg",256,256)
-            summ(2)
-            tr(2)
-            quant("eg",0,256)
-            inter("S","e0",0,256)
-            inter("V","e0",256,256)
             tq(0)
+            summ(2)
             mm0(0)
-            tq(1)
-            mm0(1)
-            tcopy("S",2)
-            oc0("S",0)
-            st0(0)
-            oc0("S",1)
-            st0(1)
+            fwd(2)
+            tcopy("S", 1)
+            oc0("S", 0)
+            tcopy("S", 2)
             mask(3)
-            quant("e0",256,256)
+            tq(1)
             summ(3)
-            tr(3)
-            d_inter("S",0,0,256)
-            tcopy("S",3)
+            mm0(1)
+            fwd(3)
+            fmm(4)
+            oc0("S", 1)
+            st0(0, 2)
+            tcopy("S", 3)
             mask(4)
             tq(2)
+            ftr(4)
             mm0(2)
-            summ(4)
-            tr(4)
-            oc0("S",2)
-            st0(2)
-            tcopy("S",4)
+            fmm(5)
             mask(5)
-            quant("e0",0,256)
-            summ(5)
-            tr(5)
             tq(3)
+            ftr(5)
+            tcopy("S", 4)
+            oc0("S", 2)
+            tcopy("S", 5)
             mm0(3)
-            d_inter("S",0,256,256)
-            oc0("S",3)
-            st0(3)
-            tcopy("S",5)
-            inter("V","e1",256,256)
-            tq(4)
-            mm0(4)
+            fmm(6)
+            quant("e0", 0, 512)
             mask(6)
-            quant("d0",0,256)
-            summ(6)
-            tr(6)
-            mm1(0,0)
-            mm1(0,1)
-            oc0("S",4)
-            st0(4)
-            tcopy("S",6)
-            inter("V","e1",0,256)
-            tq(5)
-            mm0(5)
-            oc0("S",5)
-            st0(5)
+            tq(4)
+            ftr(6)
+            fmm(7)
+            oc0("S", 3)
+            st0(2, 2)
+            tcopy("S", 6)
             mask(7)
-            quant("e1",256,256)
-            summ(7)
-            tr(7)
-            quant("e1",0,256)
-            tcopy("S",7)
-            d_inter("V",1,0,128)
+            tq(5)
+            ftr(7)
+            mm0(4)
+            mm0(5)
+            tcopy("S", 7)
+            back(4)
+            back(5)
+            back(6)
+            back(7)
+            d_inter("V", 0, 0, 512)
             tq(6)
-            mm0(6)
-            d_inter("V",1,128,128)
-            quant("d1",0,128)
-            mm1(1,0)
-            oc0("S",6)
-            st0(6)
-            quant("d0",256,256)
-            quant("d1",128,128)
-            mm1(1,1)
-            mm1(0,2)
-            mm1(0,3)
-            oc1("S",0)
-            st1(0)
-            d_inter("V",1,256,128)
             tq(7)
+            oc0("S", 4)
+            oc0("S", 5)
+            st0(4, 2)
+            mm0(6)
             mm0(7)
-            d_inter("V",1,384,128)
-            quant("d1",256,128)
-            mm1(1,2)
-            oc1("S",1)
-            st1(1)
-            quant("d1",384,128)
-            mm1(1,3)
-            oc0("S",7)
-            st0(7)
-            oc1("V",2)
-            st1(2)
-            oc1("S",3)
-            st1(3)
+            inter("V", "e1", 0, 512)
+            quant("d0", 0, 512)
+            quant("e1", 0, 512)
+            bcopy("S", 1, 0)
+            bcopy("S", 1, 1)
+            oc0("S", 6)
+            oc0("S", 7)
+            st0(6, 2)
+            quant("d1", 0, 256)
+            mm1(0)
+            mm1(1)
+            bcopy("V", 1, 2)
+            bcopy("V", 1, 3)
+            oc1("S", 0)
+            oc1("S", 1)
+            st1(0, 2)
+            quant("d1", 256, 256)
+            mm1(2)
+            mm1(3)
+            oc1("S", 2)
+            oc1("V", 3)
+            st1(2, 1)
+            st1(3, 1)

@@ -19,7 +19,11 @@ TOKENS = 1024
 UNITS = 8
 FLOPS = 2 * 2 * TOKENS * N * N
 BYTES = TOKENS * N * (4 + 2 + 2 + 2) + N * N * 2 + TOKENS * N * 4 + N * N * 4
-VUNITS = (0, 1, 2, 3)
+VUNITS = (4, 5, 6, 7)
+T_BANK = (0, 1, 0, 1, 0, 1, 0, 1)
+B_BANK = ((2, 3), (2, 3))
+O0_BANK = (4, 5, 4, 5, 4, 5, 4, 5)
+O1_BANK = (6, 7, 0, 1)
 
 
 def tile_bspncn_pb_v_kernel(tc, e_gen2, e_disc2, e_gen1, e_disc3, j2, v2, x2, Eg1, Ed2, v_pre, grad_out, out_0, out_1):
@@ -33,9 +37,10 @@ def tile_bspncn_pb_v_kernel(tc, e_gen2, e_disc2, e_gen1, e_disc3, j2, v2, x2, Eg
 
     with ExitStack() as ctx:
         keep = ctx.enter_context(tc.tile_pool(name="keep", bufs=1))
-        t_psum = ctx.enter_context(tc.psum_pool(name="t_psum", bufs=2))
-        b_psum = ctx.enter_context(tc.psum_pool(name="b_psum", bufs=1))
-        o_psum = ctx.enter_context(tc.psum_pool(name="o_psum", bufs=4))
+        psum = ctx.enter_context(tc.psum_pool(name="psum", bufs=1))
+
+        def bank(i, shape):
+            return psum.tile(shape, F32, name=f"bank{i}")
 
         def sb(name, shape, dtype):
             return keep.tile(shape, dtype, name=name, align_bytes=64)
@@ -46,7 +51,7 @@ def tile_bspncn_pb_v_kernel(tc, e_gen2, e_disc2, e_gen1, e_disc3, j2, v2, x2, Eg
         g_t = [sb(f"g{k}", [P, 2 * N], BF16) for k in range(UNITS)]
         m_t = {k: sb(f"m{k}", [P, N], BF16) for k in VUNITS}
         s_all = sb("s_all", [P, PACK, N], F32)
-        s_t = [s_all[:, j, :] for j in range(PACK)] + [sb(f"s{k}", [P, N], F32)[:] for k in range(PACK)]
+        s_t = [sb(f"s{k}", [P, N], F32)[:] for k in range(PACK)] + [s_all[:, j, :] for j in range(PACK)]
         raw = {n: sb(f"raw_{n}", [P, PACK, N], BF16) for n in ("eg", "e0", "e1")}
         names = ("eg", "e0", "e1", "d0", "d1")
         grouped = {n: sb(f"grp_{n}", [P, N, PACK], BF16) for n in names}
@@ -115,20 +120,21 @@ def tile_bspncn_pb_v_kernel(tc, e_gen2, e_disc2, e_gen1, e_disc3, j2, v2, x2, Eg
         tps = {}
 
         def fwd(k):
-            tp = t_psum.tile([P, PACK, P], F32, name="tp")
+            tp = bank(T_BANK[k], [P, PACK, P])
             tps[k] = tp
-            for t in range(PACK):
+            nc.tensor.matmul(tp[:, 0, :], lhsT=s_t[k][:, 0:P], rhs=ident[:], start=True, stop=True)
+            for t in range(1, PACK):
                 nc.tensor.transpose(tp[:, t, :], s_t[k][:, P * t:P * t + P], ident[:])
 
         def fmm(k):
-            tp = t_psum.tile([P, PACK, P], F32, name="tp")
+            tp = bank(T_BANK[k], [P, PACK, P])
             tps[k] = tp
             for t in range(PACK):
                 nc.tensor.matmul(tp[:, t, :], lhsT=g_t[k][:, t:N:PACK], rhs=ident20[:], start=(t == 0), stop=False)
 
         def ftr(k):
             for t in range(PACK):
-                nc.tensor.matmul(tps[k][:, t, :], lhsT=s_t[k][:, P * t:P * t + P], rhs=ident[:], is_transpose=True,
+                nc.tensor.matmul(tps[k][:, t, :], lhsT=s_t[k][:, P * t:P * t + P], rhs=ident[:], is_transpose=(t > 0),
                                  start=False, stop=(t == PACK - 1))
 
         def tcopy(eng, k):
@@ -147,7 +153,7 @@ def tile_bspncn_pb_v_kernel(tc, e_gen2, e_disc2, e_gen1, e_disc3, j2, v2, x2, Eg
         def back(k):
             if k % PACK == 0:
                 for u in range(2):
-                    bps[k // PACK, u] = b_psum.tile([P, PACK, P], F32, name=f"bp{u}")
+                    bps[k // PACK, u] = bank(B_BANK[k // PACK][u], [P, PACK, P])
             words = x_t[k][:].bitcast(F32)
             for u in range(2):
                 nc.tensor.transpose(bps[k // PACK, u][:, k % PACK, :], words[:, u:2 * P:2], ident[:])
@@ -159,7 +165,7 @@ def tile_bspncn_pb_v_kernel(tc, e_gen2, e_disc2, e_gen1, e_disc3, j2, v2, x2, Eg
         o0s = {}
 
         def mm0(k):
-            op = o_psum.tile([P, N], F32, name="op")
+            op = bank(O0_BANK[k], [P, N])
             o0s[k] = op
             nc.tensor.matmul_mx(out=op[:], lhsT=xc[k][:].bitcast(E5M2), lhsT_scale=xs[k][:],
                                 rhs=codes["eg"][:].bitcast(E4M3), rhs_scale=scales["eg"][:], start=True, stop=True)
@@ -172,13 +178,12 @@ def tile_bspncn_pb_v_kernel(tc, e_gen2, e_disc2, e_gen1, e_disc3, j2, v2, x2, Eg
 
         o1s = {}
 
-        def mm1(t):
-            op = o_psum.tile([P, N], F32, name="op")
-            o1s[t] = op
+        def mm1(g, t):
+            if g == 0:
+                o1s[t] = bank(O1_BANK[t], [P, N])
             c = slice(P * t, P * t + P)
-            for g in range(2):
-                nc.tensor.matmul_mx(out=op[:], lhsT=codes[f"d{g}"][:, c].bitcast(E5M2), lhsT_scale=scales[f"d{g}"][:, c],
-                                    rhs=codes[f"e{g}"][:].bitcast(E4M3), rhs_scale=scales[f"e{g}"][:], start=(g == 0), stop=(g == 1))
+            nc.tensor.matmul_mx(out=o1s[t][:], lhsT=codes[f"d{g}"][:, c].bitcast(E5M2), lhsT_scale=scales[f"d{g}"][:, c],
+                                rhs=codes[f"e{g}"][:].bitcast(E4M3), rhs_scale=scales[f"e{g}"][:], start=(g == 0), stop=(g == 1))
 
         def oc1(eng, t):
             copy(eng, r1[t // 2][:, t % 2, :], o1s[t][:])
@@ -189,101 +194,115 @@ def tile_bspncn_pb_v_kernel(tc, e_gen2, e_disc2, e_gen1, e_disc3, j2, v2, x2, Eg
         make_identity(nc, ident[:])
         with tc.manual_schedule():
             load_w("eg")
-            load_g(0)
-            load_v(0, 1)
-            load_w("e0")
-            for k in range(1, UNITS):
+            for k in range(UNITS):
                 load_g(k)
                 load_v(k, 1)
-            load_w("e1")
+                if k < 2:
+                    load_w(f"e{k}")
             nc.scalar.activation(out=ident20[:], in_=ident[:], func=COPY, scale=20.0)
-            inter("S", "eg", 256, 256)
-            inter("V", "eg", 0, 256)
+            inter("S", "eg", 192, 320)
+            inter("V", "eg", 0, 192)
+            fmm(0)
             mask(0)
+            ftr(0)
+            fmm(1)
             quant("eg", 0, 512)
-            summ(0)
-            fwd(0)
-            inter("S", "e0", 0, 512)
+            inter("S", "e0", 320, 192)
+            inter("V", "e0", 0, 320)
             tcopy("S", 0)
             mask(1)
-            summ(1)
-            fwd(1)
-            mask(2)
+            ftr(1)
             tq(0)
-            summ(2)
             mm0(0)
-            fwd(2)
+            back(0)
+            fmm(2)
+            quant("e0", 0, 512)
             tcopy("S", 1)
+            inter("S", "e1", 320, 192)
+            inter("V", "e1", 0, 320)
+            back(1)
             oc0("S", 0)
-            tcopy("S", 2)
-            mask(3)
+            mask(2)
+            ftr(2)
+            fmm(3)
             tq(1)
-            summ(3)
             mm0(1)
-            fwd(3)
-            fmm(4)
+            quant("e1", 0, 512)
+            tcopy("S", 2)
             oc0("S", 1)
             st0(0, 2)
+            mask(3)
+            ftr(3)
+            back(2)
             tcopy("S", 3)
             mask(4)
             tq(2)
-            ftr(4)
+            summ(4)
             mm0(2)
-            fmm(5)
+            fwd(4)
+            back(3)
+            oc0("S", 2)
+            tcopy("S", 4)
             mask(5)
             tq(3)
-            ftr(5)
-            tcopy("S", 4)
-            oc0("S", 2)
-            tcopy("S", 5)
+            summ(5)
             mm0(3)
-            fmm(6)
-            quant("e0", 0, 512)
-            mask(6)
-            tq(4)
-            ftr(6)
-            fmm(7)
+            fwd(5)
             oc0("S", 3)
             st0(2, 2)
+            tcopy("S", 5)
+            mask(6)
+            tq(4)
+            summ(6)
+            mm0(4)
+            fwd(6)
+            oc0("S", 4)
+            st0(4, 1)
             tcopy("S", 6)
             mask(7)
             tq(5)
-            ftr(7)
-            mm0(4)
+            summ(7)
             mm0(5)
-            tcopy("S", 7)
-            back(4)
-            back(5)
-            back(6)
-            back(7)
-            d_inter("V", 0, 0, 512)
-            tq(6)
-            tq(7)
-            oc0("S", 4)
+            fwd(7)
             oc0("S", 5)
-            st0(4, 2)
+            st0(5, 1)
+            tcopy("S", 7)
+            bcopy("V", 0, 0)
+            d_inter("V", 1, 0, 128)
+            tq(6)
             mm0(6)
-            mm0(7)
-            inter("V", "e1", 0, 512)
-            quant("d0", 0, 512)
-            quant("e1", 0, 512)
-            bcopy("S", 1, 0)
-            bcopy("S", 1, 1)
+            quant("d0", 0, 128)
+            mm1(0, 0)
+            quant("d1", 0, 128)
+            mm1(1, 0)
+            bcopy("S", 0, 2)
+            bcopy("S", 0, 3)
             oc0("S", 6)
-            oc0("S", 7)
-            st0(6, 2)
-            quant("d1", 0, 256)
-            mm1(0)
-            mm1(1)
-            bcopy("V", 1, 2)
-            bcopy("V", 1, 3)
+            st0(6, 1)
             oc1("S", 0)
+            st1(0, 1)
+            bcopy("V", 0, 1)
+            tq(7)
+            mm0(7)
+            d_inter("V", 1, 128, 128)
+            quant("d0", 128, 128)
+            mm1(0, 1)
+            quant("d1", 128, 128)
+            mm1(1, 1)
+            oc0("S", 7)
+            st0(7, 1)
             oc1("S", 1)
-            st1(0, 2)
-            quant("d1", 256, 256)
-            mm1(2)
-            mm1(3)
+            st1(1, 1)
+            d_inter("V", 1, 256, 128)
+            quant("d0", 256, 256)
+            mm1(0, 2)
+            mm1(0, 3)
+            d_inter("V", 1, 384, 128)
+            quant("d1", 256, 128)
+            mm1(1, 2)
+            quant("d1", 384, 128)
+            mm1(1, 3)
             oc1("S", 2)
-            oc1("V", 3)
             st1(2, 1)
+            oc1("V", 3)
             st1(3, 1)

@@ -194,11 +194,13 @@ def tile_bspncn_pb_v_kernel(tc, e_gen2, e_disc2, e_gen1, e_disc3, j2, v2, x2, Eg
         make_identity(nc, ident[:])
         with tc.manual_schedule():
             load_w("eg")
-            for k in range(UNITS):
+            load_g(0)
+            load_v(0, 1)
+            load_w("e0")
+            for k in range(1, UNITS):
                 load_g(k)
                 load_v(k, 1)
-                if k < 2:
-                    load_w(f"e{k}")
+            load_w("e1")
             nc.scalar.activation(out=ident20[:], in_=ident[:], func=COPY, scale=20.0)
             inter("S", "eg", 192, 320)
             inter("V", "eg", 0, 192)
@@ -207,32 +209,29 @@ def tile_bspncn_pb_v_kernel(tc, e_gen2, e_disc2, e_gen1, e_disc3, j2, v2, x2, Eg
             ftr(0)
             fmm(1)
             quant("eg", 0, 512)
-            inter("S", "e0", 320, 192)
-            inter("V", "e0", 0, 320)
+            inter("S", "e0", 256, 256)
+            inter("V", "e0", 0, 256)
             tcopy("S", 0)
             mask(1)
             ftr(1)
+            fmm(2)
+            quant("e0", 0, 512)
             tq(0)
             mm0(0)
             back(0)
-            fmm(2)
-            quant("e0", 0, 512)
             tcopy("S", 1)
-            inter("S", "e1", 320, 192)
-            inter("V", "e1", 0, 320)
-            back(1)
             oc0("S", 0)
             mask(2)
             ftr(2)
             fmm(3)
             tq(1)
             mm0(1)
-            quant("e1", 0, 512)
             tcopy("S", 2)
             oc0("S", 1)
             st0(0, 2)
             mask(3)
             ftr(3)
+            back(1)
             back(2)
             tcopy("S", 3)
             mask(4)
@@ -248,6 +247,7 @@ def tile_bspncn_pb_v_kernel(tc, e_gen2, e_disc2, e_gen1, e_disc3, j2, v2, x2, Eg
             summ(5)
             mm0(3)
             fwd(5)
+            bcopy("S", 0, 0)
             oc0("S", 3)
             st0(2, 2)
             tcopy("S", 5)
@@ -256,8 +256,8 @@ def tile_bspncn_pb_v_kernel(tc, e_gen2, e_disc2, e_gen1, e_disc3, j2, v2, x2, Eg
             summ(6)
             mm0(4)
             fwd(6)
+            bcopy("S", 0, 1)
             oc0("S", 4)
-            st0(4, 1)
             tcopy("S", 6)
             mask(7)
             tq(5)
@@ -265,34 +265,32 @@ def tile_bspncn_pb_v_kernel(tc, e_gen2, e_disc2, e_gen1, e_disc3, j2, v2, x2, Eg
             mm0(5)
             fwd(7)
             oc0("S", 5)
-            st0(5, 1)
+            st0(4, 2)
             tcopy("S", 7)
-            bcopy("V", 0, 0)
-            d_inter("V", 1, 0, 128)
+            inter("V", "e1", 0, 512)
             tq(6)
             mm0(6)
-            quant("d0", 0, 128)
+            quant("d0", 0, 256)
             mm1(0, 0)
-            quant("d1", 0, 128)
-            mm1(1, 0)
-            bcopy("S", 0, 2)
-            bcopy("S", 0, 3)
-            oc0("S", 6)
-            st0(6, 1)
-            oc1("S", 0)
-            st1(0, 1)
-            bcopy("V", 0, 1)
+            mm1(0, 1)
+            quant("e1", 0, 512)
             tq(7)
             mm0(7)
-            d_inter("V", 1, 128, 128)
-            quant("d0", 128, 128)
-            mm1(0, 1)
-            quant("d1", 128, 128)
-            mm1(1, 1)
+            bcopy("S", 0, 2)
+            oc0("S", 6)
+            st0(6, 1)
+            bcopy("S", 0, 3)
             oc0("S", 7)
             st0(7, 1)
+            d_inter("V", 1, 0, 128)
+            d_inter("V", 1, 128, 128)
+            quant("d1", 0, 128)
+            mm1(1, 0)
+            quant("d1", 128, 128)
+            mm1(1, 1)
+            oc1("S", 0)
             oc1("S", 1)
-            st1(1, 1)
+            st1(0, 2)
             d_inter("V", 1, 256, 128)
             quant("d0", 256, 256)
             mm1(0, 2)
@@ -302,7 +300,6 @@ def tile_bspncn_pb_v_kernel(tc, e_gen2, e_disc2, e_gen1, e_disc3, j2, v2, x2, Eg
             mm1(1, 2)
             quant("d1", 384, 128)
             mm1(1, 3)
-            oc1("S", 2)
-            st1(2, 1)
-            oc1("V", 3)
-            st1(3, 1)
+            oc1("V", 2)
+            oc1("S", 3)
+            st1(2, 2)

@@ -15,291 +15,263 @@ COPY = mybir.ActivationFunctionType.Copy
 P = 128
 PACK = 4
 N = 512
-TOKENS = 1024
-UNITS = 8
-FLOPS = 2 * 2 * TOKENS * N * N
-BYTES = TOKENS * N * (4 + 2 + 2 + 2) + N * N * 2 + TOKENS * N * 4 + N * N * 4
-VUNITS = (4, 5, 6, 7)
-T_BANK = (0, 1, 0, 1, 0, 1, 0, 1)
-B_BANK = ((2, 3), (2, 3))
-O0_BANK = (4, 5, 4, 5, 4, 5, 4, 5)
-O1_BANK = (6, 7, 0, 1)
+SAMPLES = 1024
+UNITS = SAMPLES // P
+THRESHOLD = 0.4
+GJ_WEIGHT = 20.0
+DZ_SCALE = 0.005
+
+VECTOR_COLUMNS = {"Eg1": 192, "e0": 256}
+
+TURN_BANKS = (0, 1)
+BACK_BANKS = (2, 3)
+OUT0_BANKS = (4, 5)
+OUT1_BANKS = (6, 7, 0, 1)
+WARM_BANK = 7
+
+FLOPS = 2 * 2 * SAMPLES * N * N
+BYTES = SAMPLES * N * (4 + 2 + 2 + 2) + N * N * 2 + SAMPLES * N * 4 + N * N * 4
 
 
 def tile_bspncn_pb_v_kernel(tc, e_gen2, e_disc2, e_gen1, e_disc3, j2, v2, x2, Eg1, Ed2, v_pre, grad_out, out_0, out_1):
     nc = tc.nc
-    v_hbm = v_pre.rearrange("(g p j) w -> g p j w", p=P, j=PACK)
-    g_hbm = grad_out.rearrange("(g p j) w -> g p j w", p=P, j=PACK)
-    e_hbm = e_gen1.rearrange("(g p j) w -> g p j w", p=P, j=PACK)
-    o0_hbm = out_0.rearrange("(g p j) w -> g p j w", p=P, j=PACK)
-    o1_hbm = out_1.rearrange("(q t) w -> q t w", t=PACK)
-    w_hbm = {"eg": Eg1.rearrange("(p j) w -> p j w", j=PACK), "e0": e_hbm[0], "e1": e_hbm[1]}
+    by_sample = "(g p j) w -> g p j w"
+    v_hbm = v_pre.rearrange(by_sample, p=P, j=PACK)
+    grad_hbm = grad_out.rearrange(by_sample, p=P, j=PACK)
+    e_hbm = e_gen1.rearrange(by_sample, p=P, j=PACK)
+    out0_hbm = out_0.rearrange(by_sample, p=P, j=PACK)
+    out1_hbm = out_1.rearrange("(q t) w -> q t w", t=PACK)
+    operand_hbm = {"Eg1": Eg1.rearrange("(q t) w -> q t w", t=PACK), "e0": e_hbm[0], "e1": e_hbm[1]}
 
     with ExitStack() as ctx:
-        keep = ctx.enter_context(tc.tile_pool(name="keep", bufs=1))
+        sbuf = ctx.enter_context(tc.tile_pool(name="sbuf", bufs=1))
         psum = ctx.enter_context(tc.psum_pool(name="psum", bufs=1))
+
+        def sb(name, shape, dtype):
+            return sbuf.tile(shape, dtype, name=name, align_bytes=64)
 
         def bank(i, shape):
             return psum.tile(shape, F32, name=f"bank{i}")
 
-        def sb(name, shape, dtype):
-            return keep.tile(shape, dtype, name=name, align_bytes=64)
-
         ident = sb("ident", [P, P], F32)
-        ident20 = sb("ident20", [P, P], BF16)
-        v_t = [sb(f"v{i}", [P, 2, N], F32) for i in range(UNITS // 2)]
-        g_t = [sb(f"g{k}", [P, 2 * N], BF16) for k in range(UNITS)]
-        m_t = {k: sb(f"m{k}", [P, N], BF16) for k in VUNITS}
-        s_all = sb("s_all", [P, PACK, N], F32)
-        s_t = [sb(f"s{k}", [P, N], F32)[:] for k in range(PACK)] + [s_all[:, j, :] for j in range(PACK)]
-        raw = {n: sb(f"raw_{n}", [P, PACK, N], BF16) for n in ("eg", "e0", "e1")}
-        names = ("eg", "e0", "e1", "d0", "d1")
-        grouped = {n: sb(f"grp_{n}", [P, N, PACK], BF16) for n in names}
-        codes = {n: sb(f"codes_{n}", [P, N], U32) for n in names}
-        scales = {n: sb(f"scales_{n}", [P, N], U8) for n in names}
-        x_t = [sb(f"x{k}", [P, P * PACK], BF16) for k in range(UNITS)]
-        xc = [sb(f"xc{k}", [P, P], U32) for k in range(UNITS)]
-        xs = [sb(f"xs{k}", [P, P], U8) for k in range(UNITS)]
-        r0 = [sb(f"r0{i}", [P, 2, N], F32) for i in range(4)]
-        r1 = [sb(f"r1{i}", [P, 2, N], F32) for i in range(2)]
+        ident_gj = sb("ident_gj", [P, P], BF16)
+        v_pre_sb = [sb(f"v{k}", [P, N], F32) for k in range(UNITS)]
+        grad_sb = [sb(f"grad{k}", [P, 2 * N], BF16) for k in range(UNITS)]
+        kept = [sb(f"kept{k}", [P, N], F32 if k < PACK else BF16) for k in range(UNITS)]
+        s_pass1 = sb("s_pass1", [P, PACK, N], F32)
+        loaded = {name: sb(f"loaded_{name}", [P, PACK, N], BF16) for name in operand_hbm}
+        wide = ("Eg1", "e0", "e1", "dz0", "dz1")
+        grouped = {name: sb(f"grouped_{name}", [P, N, PACK], BF16) for name in wide}
+        codes = {name: sb(f"codes_{name}", [P, N], U32) for name in wide}
+        scales = {name: sb(f"scales_{name}", [P, N], U8) for name in wide}
+        dzt = [sb(f"dzt{k}", [P, P * PACK], BF16) for k in range(UNITS)]
+        dzt_codes = [sb(f"dzt_codes{k}", [P, P], U32) for k in range(UNITS)]
+        dzt_scales = [sb(f"dzt_scales{k}", [P, P], U8) for k in range(UNITS)]
+        out0_sb = [sb(f"out0_{i}", [P, 2, N], F32) for i in range(UNITS // 2)]
+        out1_sb = [sb(f"out1_{i}", [P, 2, N], F32) for i in range(PACK // 2)]
+        turned, back, out0_ps, out1_ps = {}, {}, {}, {}
 
-        def load_v(k, n):
-            nc.sync.dma_start(out=v_t[k // 2][:, k % 2:k % 2 + n, :], in_=v_hbm[k // 4][:, k % 4:k % 4 + n, :])
+        def load_unit(k):
+            nc.sync.dma_start(out=grad_sb[k][:], in_=grad_hbm[k // PACK][:, k % PACK, 0:2 * N])
+            nc.sync.dma_start(out=v_pre_sb[k][:], in_=v_hbm[k // PACK][:, k % PACK, :])
 
-        def load_g(k):
-            nc.sync.dma_start(out=g_t[k][:], in_=g_hbm[k // 4][:, k % 4, 0:2 * N])
+        def load_operand(name):
+            nc.sync.dma_start(out=loaded[name][:], in_=operand_hbm[name])
 
-        def load_w(name):
-            nc.sync.dma_start(out=raw[name][:], in_=w_hbm[name])
+        def on_vector(out, in_):
+            nc.vector.tensor_copy(out=out, in_=in_)
 
-        def copy(eng, out, in_):
-            if eng == "V":
-                nc.vector.tensor_copy(out=out, in_=in_)
-            else:
-                nc.scalar.copy(out=out, in_=in_)
+        def on_scalar(out, in_):
+            nc.scalar.copy(out=out, in_=in_)
 
-        def four_by_four_in(ap):
+        def slots_first(ap):
             return ap.rearrange("p j (c i) -> p c j i", i=4)
 
-        def four_by_four_out(ap):
+        def slots_last(ap):
             return ap.rearrange("p (c i) j -> p c j i", i=4)
 
-        def inter(eng, name, c0, w):
-            copy(eng, four_by_four_out(grouped[name][:, c0:c0 + w, :]), four_by_four_in(raw[name][:, :, c0:c0 + w]))
+        def interleave(copy, name, c0, c1):
+            copy(slots_last(grouped[name][:, c0:c1, :]), slots_first(loaded[name][:, :, c0:c1]))
 
-        def d_inter(eng, g, c0, w):
-            out = four_by_four_out(grouped[f"d{g}"][:, c0:c0 + w, :])
-            in_ = four_by_four_in(s_all[:, :, c0:c0 + w])
-            if eng == "V":
-                nc.vector.tensor_scalar(out=out, in0=in_, scalar1=0.005, scalar2=None, op0=OP.mult)
-            else:
-                nc.scalar.activation(out=out, in_=in_, func=COPY, scale=0.005)
+        def interleave_shared(name):
+            interleave(on_scalar, name, VECTOR_COLUMNS[name], N)
+            interleave(on_vector, name, 0, VECTOR_COLUMNS[name])
 
-        def quant(name, c0, w):
-            fmt = E5M2 if name[0] == "d" else E4M3
-            nc.vector.quantize_mx(out=codes[name][:, c0:c0 + w].bitcast(fmt), scales=scales[name][:, c0:c0 + w],
-                                  in_=grouped[name][:, c0:c0 + w, :].rearrange("p w j -> p (w j)"))
-
-        def by_slot(ap):
-            return ap.rearrange("p (q t) -> p t q", t=PACK)
+        def quantize(name, c0=0, c1=N):
+            fmt = E5M2 if name.startswith("dz") else E4M3
+            nc.vector.quantize_mx(out=codes[name][:, c0:c1].bitcast(fmt), scales=scales[name][:, c0:c1],
+                                  in_=grouped[name][:, c0:c1, :].rearrange("p c j -> p (c j)"))
 
         def mask(k):
-            v = v_t[k // 2][:, k % 2, :]
-            gv = g_t[k][:, N:2 * N]
-            if k in VUNITS:
-                nc.vector.scalar_tensor_tensor(out=m_t[k][:], in0=v, scalar=0.4, in1=gv, op0=OP.is_lt, op1=OP.mult)
-            else:
-                nc.vector.scalar_tensor_tensor(out=s_t[k].rearrange("p (t q) -> p q t", t=PACK),
-                                               in0=v.rearrange("p (q t) -> p q t", t=PACK), scalar=0.4,
-                                               in1=gv.rearrange("p (q t) -> p q t", t=PACK), op0=OP.is_lt, op1=OP.mult)
+            out, v, gv = kept[k][:], v_pre_sb[k][:], grad_sb[k][:, N:2 * N]
+            if k < PACK:
+                out = out.rearrange("p (t q) -> p q t", t=PACK)
+                v, gv = (ap.rearrange("p (q t) -> p q t", t=PACK) for ap in (v, gv))
+            nc.vector.scalar_tensor_tensor(out=out, in0=v, scalar=THRESHOLD, in1=gv, op0=OP.is_lt, op1=OP.mult)
 
-        def summ(k):
-            nc.vector.scalar_tensor_tensor(out=s_t[k].rearrange("p (t q) -> p t q", t=PACK), in0=by_slot(g_t[k][:, 0:N]),
-                                           scalar=20.0, in1=by_slot(m_t[k][:]), op0=OP.mult, op1=OP.add)
-
-        tps = {}
-
-        def fwd(k):
-            tp = bank(T_BANK[k], [P, PACK, P])
-            tps[k] = tp
-            nc.tensor.matmul(tp[:, 0, :], lhsT=s_t[k][:, 0:P], rhs=ident[:], start=True, stop=True)
-            for t in range(1, PACK):
-                nc.tensor.transpose(tp[:, t, :], s_t[k][:, P * t:P * t + P], ident[:])
-
-        def fmm(k):
-            tp = bank(T_BANK[k], [P, PACK, P])
-            tps[k] = tp
+        def turn_gj(k):
+            turned[k] = bank(TURN_BANKS[k % 2], [P, PACK, P])
             for t in range(PACK):
-                nc.tensor.matmul(tp[:, t, :], lhsT=g_t[k][:, t:N:PACK], rhs=ident20[:], start=(t == 0), stop=False)
+                nc.tensor.matmul(turned[k][:, t, :], lhsT=grad_sb[k][:, t:N:PACK], rhs=ident_gj[:], start=(t == 0), stop=False)
 
-        def ftr(k):
+        def turn_kept(k):
             for t in range(PACK):
-                nc.tensor.matmul(tps[k][:, t, :], lhsT=s_t[k][:, P * t:P * t + P], rhs=ident[:], is_transpose=(t > 0),
+                nc.tensor.matmul(turned[k][:, t, :], lhsT=kept[k][:, P * t:P * (t + 1)], rhs=ident[:], is_transpose=True,
                                  start=False, stop=(t == PACK - 1))
 
-        def tcopy(eng, k):
-            out = x_t[k][:].rearrange("q (p t) -> q p t", t=PACK)
-            in_ = tps[k][:].rearrange("q t p -> q p t")
-            if eng == "V":
-                nc.vector.tensor_scalar(out=out, in0=in_, scalar1=0.005, scalar2=None, op0=OP.mult)
-            else:
-                nc.scalar.activation(out=out, in_=in_, func=COPY, scale=0.005)
+        def add_on_vector(k):
+            gj, kept_gv = (ap.rearrange("p (q t) -> p t q", t=PACK) for ap in (grad_sb[k][:, 0:N], kept[k][:]))
+            nc.vector.scalar_tensor_tensor(out=s_pass1[:, k % PACK, :].rearrange("p (t q) -> p t q", t=PACK), in0=gj,
+                                           scalar=GJ_WEIGHT, in1=kept_gv, op0=OP.mult, op1=OP.add)
 
-        def tq(k):
-            nc.vector.quantize_mx(out=xc[k][:].bitcast(E5M2), scales=xs[k][:], in_=x_t[k][:])
+        def turn_sum(k):
+            turned[k] = bank(TURN_BANKS[k % 2], [P, PACK, P])
+            for t in range(PACK):
+                nc.tensor.transpose(turned[k][:, t, :], s_pass1[:, k % PACK, P * t:P * (t + 1)], ident[:])
 
-        bps = {}
+        def round_turned(k):
+            nc.scalar.activation(out=dzt[k][:].rearrange("q (p t) -> q p t", t=PACK),
+                                 in_=turned[k][:].rearrange("q t p -> q p t"), func=COPY, scale=DZ_SCALE)
 
-        def back(k):
-            if k % PACK == 0:
+        def round_pass1(t):
+            c = slice(P * t, P * (t + 1))
+            nc.vector.tensor_scalar(out=slots_last(grouped["dz1"][:, c, :]), in0=slots_first(s_pass1[:, :, c]),
+                                    scalar1=DZ_SCALE, scalar2=None, op0=OP.mult)
+
+        def turn_back(k):
+            if k == 0:
                 for u in range(2):
-                    bps[k // PACK, u] = bank(B_BANK[k // PACK][u], [P, PACK, P])
-            words = x_t[k][:].bitcast(F32)
+                    back[u] = bank(BACK_BANKS[u], [P, PACK, P])
+            words = dzt[k][:].bitcast(F32)
             for u in range(2):
-                nc.tensor.transpose(bps[k // PACK, u][:, k % PACK, :], words[:, u:2 * P:2], ident[:])
+                nc.tensor.transpose(back[u][:, k, :], words[:, u:2 * P:2], ident[:])
 
-        def bcopy(eng, g, t):
-            halves = bps[g, t // 2][:].rearrange("p j q -> p (j q)").bitcast(BF16).rearrange("p (j q e) -> p e q j", j=PACK, e=2)
-            copy(eng, grouped[f"d{g}"][:, P * t:P * t + P, :], halves[:, t % 2, :, :])
+        def copy_back(t):
+            halves = back[t // 2][:].rearrange("p j q -> p (j q)").bitcast(BF16).rearrange("p (j q e) -> p e q j", j=PACK, e=2)
+            on_scalar(grouped["dz0"][:, P * t:P * (t + 1), :], halves[:, t % 2, :, :])
 
-        o0s = {}
+        def times_Eg1(k, out):
+            nc.tensor.matmul_mx(out=out, lhsT=dzt_codes[k][:].bitcast(E5M2), lhsT_scale=dzt_scales[k][:],
+                                rhs=codes["Eg1"][:].bitcast(E4M3), rhs_scale=scales["Eg1"][:], start=True, stop=True)
 
-        def mm0(k):
-            op = bank(O0_BANK[k], [P, N])
-            o0s[k] = op
-            nc.tensor.matmul_mx(out=op[:], lhsT=xc[k][:].bitcast(E5M2), lhsT_scale=xs[k][:],
-                                rhs=codes["eg"][:].bitcast(E4M3), rhs_scale=scales["eg"][:], start=True, stop=True)
+        def out0_product(k):
+            nc.vector.quantize_mx(out=dzt_codes[k][:].bitcast(E5M2), scales=dzt_scales[k][:], in_=dzt[k][:])
+            out0_ps[k] = bank(OUT0_BANKS[k % 2], [P, N])
+            times_Eg1(k, out0_ps[k][:])
 
-        def oc0(eng, k):
-            copy(eng, r0[k // 2][:, k % 2, :], o0s[k][:])
+        def out0_copy(k):
+            on_scalar(out0_sb[k // 2][:, k % 2, :], out0_ps[k][:])
 
-        def st0(k, n):
-            nc.sync.dma_start(out=o0_hbm[k // 4][:, k % 4:k % 4 + n, :], in_=r0[k // 2][:, k % 2:k % 2 + n, :])
+        def out0_store(k, n):
+            nc.sync.dma_start(out=out0_hbm[k // PACK][:, k % PACK:k % PACK + n, :], in_=out0_sb[k // 2][:, k % 2:k % 2 + n, :])
 
-        o1s = {}
-
-        def mm1(g, t):
+        def out1_product(g, t):
             if g == 0:
-                o1s[t] = bank(O1_BANK[t], [P, N])
-            c = slice(P * t, P * t + P)
-            nc.tensor.matmul_mx(out=o1s[t][:], lhsT=codes[f"d{g}"][:, c].bitcast(E5M2), lhsT_scale=scales[f"d{g}"][:, c],
+                out1_ps[t] = bank(OUT1_BANKS[t], [P, N])
+            c = slice(P * t, P * (t + 1))
+            nc.tensor.matmul_mx(out=out1_ps[t][:], lhsT=codes[f"dz{g}"][:, c].bitcast(E5M2), lhsT_scale=scales[f"dz{g}"][:, c],
                                 rhs=codes[f"e{g}"][:].bitcast(E4M3), rhs_scale=scales[f"e{g}"][:], start=(g == 0), stop=(g == 1))
 
-        def oc1(eng, t):
-            copy(eng, r1[t // 2][:, t % 2, :], o1s[t][:])
+        def out1_pass0(t):
+            quantize("dz0", P * t, P * (t + 2))
+            out1_product(0, t)
+            out1_product(0, t + 1)
 
-        def st1(t, n):
-            nc.sync.dma_start(out=o1_hbm[:, t:t + n, :], in_=r1[t // 2][:, t % 2:t % 2 + n, :])
+        def out1_pass1(t):
+            quantize("dz1", P * t, P * (t + 1))
+            out1_product(1, t)
+
+        def out1_copy(copy, t):
+            copy(out1_sb[t // 2][:, t % 2, :], out1_ps[t][:])
+
+        def out1_store(t):
+            nc.sync.dma_start(out=out1_hbm[:, t:t + 2, :], in_=out1_sb[t // 2][:])
+
+        def warm_up_plain(name):
+            idle = bank(WARM_BANK, [P, N])
+            nc.tensor.matmul(idle[:], lhsT=ident_gj[:], rhs=loaded[name][:, 0, :], start=True, stop=True)
+
+        def warm_up_mx(k):
+            idle = bank(WARM_BANK, [P, N])
+            times_Eg1(k, idle[:])
 
         make_identity(nc, ident[:])
         with tc.manual_schedule():
-            load_w("eg")
-            load_g(0)
-            load_v(0, 1)
-            load_w("e0")
+            load_operand("Eg1")
+            load_unit(0)
+            load_operand("e0")
             for k in range(1, UNITS):
-                load_g(k)
-                load_v(k, 1)
-            load_w("e1")
-            nc.scalar.activation(out=ident20[:], in_=ident[:], func=COPY, scale=20.0)
-            inter("S", "eg", 192, 320)
-            inter("V", "eg", 0, 192)
-            fmm(0)
+                load_unit(k)
+            load_operand("e1")
+            nc.scalar.activation(out=ident_gj[:], in_=ident[:], func=COPY, scale=GJ_WEIGHT)
+
+            interleave_shared("Eg1")
+            warm_up_plain("Eg1")
+            turn_gj(0)
             mask(0)
-            ftr(0)
-            fmm(1)
-            quant("eg", 0, 512)
-            inter("S", "e0", 256, 256)
-            inter("V", "e0", 0, 256)
-            tcopy("S", 0)
+            turn_kept(0)
+            warm_up_plain("e0")
+            turn_gj(1)
+            quantize("Eg1")
+            interleave_shared("e0")
+            round_turned(0)
             mask(1)
-            ftr(1)
-            fmm(2)
-            quant("e0", 0, 512)
-            tq(0)
-            mm0(0)
-            back(0)
-            tcopy("S", 1)
-            oc0("S", 0)
+            turn_kept(1)
+            turn_gj(2)
+            quantize("e0")
+            out0_product(0)
+            turn_back(0)
+            round_turned(1)
+            out0_copy(0)
             mask(2)
-            ftr(2)
-            fmm(3)
-            tq(1)
-            mm0(1)
-            tcopy("S", 2)
-            oc0("S", 1)
-            st0(0, 2)
+            turn_kept(2)
+            turn_gj(3)
+            out0_product(1)
+            round_turned(2)
+            out0_copy(1)
+            out0_store(0, 2)
             mask(3)
-            ftr(3)
-            back(1)
-            back(2)
-            tcopy("S", 3)
-            mask(4)
-            tq(2)
-            summ(4)
-            mm0(2)
-            fwd(4)
-            back(3)
-            oc0("S", 2)
-            tcopy("S", 4)
-            mask(5)
-            tq(3)
-            summ(5)
-            mm0(3)
-            fwd(5)
-            bcopy("S", 0, 0)
-            oc0("S", 3)
-            st0(2, 2)
-            tcopy("S", 5)
-            mask(6)
-            tq(4)
-            summ(6)
-            mm0(4)
-            fwd(6)
-            bcopy("S", 0, 1)
-            oc0("S", 4)
-            tcopy("S", 6)
-            mask(7)
-            tq(5)
-            summ(7)
-            mm0(5)
-            fwd(7)
-            oc0("S", 5)
-            st0(4, 2)
-            tcopy("S", 7)
-            inter("V", "e1", 0, 512)
-            tq(6)
-            mm0(6)
-            quant("d0", 0, 256)
-            mm1(0, 0)
-            mm1(0, 1)
-            quant("e1", 0, 512)
-            tq(7)
-            mm0(7)
-            bcopy("S", 0, 2)
-            oc0("S", 6)
-            st0(6, 1)
-            bcopy("S", 0, 3)
-            oc0("S", 7)
-            st0(7, 1)
-            d_inter("V", 1, 0, 128)
-            d_inter("V", 1, 128, 128)
-            quant("d1", 0, 128)
-            mm1(1, 0)
-            quant("d1", 128, 128)
-            mm1(1, 1)
-            oc1("S", 0)
-            oc1("S", 1)
-            st1(0, 2)
-            d_inter("V", 1, 256, 128)
-            quant("d0", 256, 256)
-            mm1(0, 2)
-            mm1(0, 3)
-            d_inter("V", 1, 384, 128)
-            quant("d1", 256, 128)
-            mm1(1, 2)
-            quant("d1", 384, 128)
-            mm1(1, 3)
-            oc1("V", 2)
-            oc1("S", 3)
-            st1(2, 2)
+            turn_kept(3)
+            turn_back(1)
+            turn_back(2)
+            round_turned(3)
+
+            for k in range(PACK, UNITS):
+                mask(k)
+                out0_product(k - 2)
+                add_on_vector(k)
+                warm_up_mx(k - 2)
+                turn_sum(k)
+                if k == PACK:
+                    turn_back(PACK - 1)
+                elif k < UNITS - 1:
+                    copy_back(k - PACK - 1)
+                out0_copy(k - 2)
+                if k % 2 == 1:
+                    out0_store(k - 3, 2)
+                round_turned(k)
+
+            interleave(on_vector, "e1", 0, N)
+            out0_product(UNITS - 2)
+            out1_pass0(0)
+            quantize("e1")
+            out0_product(UNITS - 1)
+            for i in range(2):
+                copy_back(2 + i)
+                out0_copy(UNITS - 2 + i)
+                out0_store(UNITS - 2 + i, 1)
+            round_pass1(0)
+            round_pass1(1)
+            out1_pass1(0)
+            out1_pass1(1)
+            out1_copy(on_scalar, 0)
+            out1_copy(on_scalar, 1)
+            out1_store(0)
+            round_pass1(2)
+            out1_pass0(2)
+            round_pass1(3)
+            out1_pass1(2)
+            out1_pass1(3)
+            out1_copy(on_vector, 2)
+            out1_copy(on_scalar, 3)
+            out1_store(2)

@@ -17,16 +17,16 @@ PACK = 4
 N = 512
 SAMPLES = 1024
 UNITS = SAMPLES // P
+HALF = N // 2
 THRESHOLD = 0.4
 GJ_WEIGHT = 20.0
 DZ_SCALE = 0.005
 
-VECTOR_COLUMNS = {"Eg1": 192, "e0": 256}
-
-TURN_BANKS = (0, 1)
-BACK_BANKS = (2, 3)
-OUT0_BANKS = (4, 5)
-OUT1_BANKS = (6, 7, 0, 1)
+LOWER = (2,2)
+TURN_BANKS = (0,1,0,1,0,1,0,1)
+BACK_BANKS = ((2,), (3,))
+OUT0_BANKS = (4,5)
+OUT1_BANKS = (2,0,6,7)
 WARM_BANK = 7
 
 FLOPS = 2 * 2 * SAMPLES * N * N
@@ -57,8 +57,8 @@ def tile_bspncn_pb_v_kernel(tc, e_gen2, e_disc2, e_gen1, e_disc3, j2, v2, x2, Eg
         ident_gj = sb("ident_gj", [P, P], BF16)
         v_pre_sb = [sb(f"v{k}", [P, N], F32) for k in range(UNITS)]
         grad_sb = [sb(f"grad{k}", [P, 2 * N], BF16) for k in range(UNITS)]
-        kept = [sb(f"kept{k}", [P, N], F32 if k < PACK else BF16) for k in range(UNITS)]
-        s_pass1 = sb("s_pass1", [P, PACK, N], F32)
+        kept = [sb(f"kept{k}", [P, N], F32) for k in range(UNITS)]
+        s_upper = [sb(f"s_upper{g}", [P, PACK, N - P * LOWER[g]], F32) if LOWER[g] < PACK else None for g in range(2)]
         loaded = {name: sb(f"loaded_{name}", [P, PACK, N], BF16) for name in operand_hbm}
         wide = ("Eg1", "e0", "e1", "dz0", "dz1")
         grouped = {name: sb(f"grouped_{name}", [P, N, PACK], BF16) for name in wide}
@@ -93,74 +93,77 @@ def tile_bspncn_pb_v_kernel(tc, e_gen2, e_disc2, e_gen1, e_disc3, j2, v2, x2, Eg
         def interleave(copy, name, c0, c1):
             copy(slots_last(grouped[name][:, c0:c1, :]), slots_first(loaded[name][:, :, c0:c1]))
 
-        def interleave_shared(name):
-            interleave(on_scalar, name, VECTOR_COLUMNS[name], N)
-            interleave(on_vector, name, 0, VECTOR_COLUMNS[name])
-
         def quantize(name, c0=0, c1=N):
             fmt = E5M2 if name.startswith("dz") else E4M3
             nc.vector.quantize_mx(out=codes[name][:, c0:c1].bitcast(fmt), scales=scales[name][:, c0:c1],
                                   in_=grouped[name][:, c0:c1, :].rearrange("p c j -> p (c j)"))
 
         def mask(k):
-            out, v, gv = kept[k][:], v_pre_sb[k][:], grad_sb[k][:, N:2 * N]
-            if k < PACK:
-                out = out.rearrange("p (t q) -> p q t", t=PACK)
-                v, gv = (ap.rearrange("p (q t) -> p q t", t=PACK) for ap in (v, gv))
-            nc.vector.scalar_tensor_tensor(out=out, in0=v, scalar=THRESHOLD, in1=gv, op0=OP.is_lt, op1=OP.mult)
+            v, gv = (ap.rearrange("p (q t) -> p q t", t=PACK) for ap in (v_pre_sb[k][:], grad_sb[k][:, N:2 * N]))
+            nc.vector.scalar_tensor_tensor(out=kept[k][:].rearrange("p (t q) -> p q t", t=PACK), in0=v, scalar=THRESHOLD,
+                                           in1=gv, op0=OP.is_lt, op1=OP.mult)
+
+        def add_upper(k):
+            low = LOWER[k // PACK]
+            gj = grad_sb[k][:, 0:N].rearrange("p (q t) -> p t q", t=PACK)[:, low:PACK, :]
+            nc.vector.scalar_tensor_tensor(out=s_upper[k // PACK][:, k % PACK, :].rearrange("p (t q) -> p t q", q=P), in0=gj,
+                                           scalar=GJ_WEIGHT, in1=kept[k][:, P * low:N].rearrange("p (t q) -> p t q", q=P),
+                                           op0=OP.mult, op1=OP.add)
 
         def turn_gj(k):
-            turned[k] = bank(TURN_BANKS[k % 2], [P, PACK, P])
-            for t in range(PACK):
+            turned[k] = bank(TURN_BANKS[k], [P, PACK, P])
+            for t in range(LOWER[k // PACK]):
                 nc.tensor.matmul(turned[k][:, t, :], lhsT=grad_sb[k][:, t:N:PACK], rhs=ident_gj[:], start=(t == 0), stop=False)
 
         def turn_kept(k):
-            for t in range(PACK):
+            low = LOWER[k // PACK]
+            for t in range(low):
                 nc.tensor.matmul(turned[k][:, t, :], lhsT=kept[k][:, P * t:P * (t + 1)], rhs=ident[:], is_transpose=True,
-                                 start=False, stop=(t == PACK - 1))
+                                 start=False, stop=(t == low - 1))
 
-        def add_on_vector(k):
-            gj, kept_gv = (ap.rearrange("p (q t) -> p t q", t=PACK) for ap in (grad_sb[k][:, 0:N], kept[k][:]))
-            nc.vector.scalar_tensor_tensor(out=s_pass1[:, k % PACK, :].rearrange("p (t q) -> p t q", t=PACK), in0=gj,
-                                           scalar=GJ_WEIGHT, in1=kept_gv, op0=OP.mult, op1=OP.add)
-
-        def turn_sum(k):
-            turned[k] = bank(TURN_BANKS[k % 2], [P, PACK, P])
-            for t in range(PACK):
-                nc.tensor.transpose(turned[k][:, t, :], s_pass1[:, k % PACK, P * t:P * (t + 1)], ident[:])
+        def turn_upper(k):
+            low = LOWER[k // PACK]
+            for t in range(low, PACK):
+                nc.tensor.transpose(turned[k][:, t, :], s_upper[k // PACK][:, k % PACK, P * (t - low):P * (t - low + 1)], ident[:])
 
         def round_turned(k):
             nc.scalar.activation(out=dzt[k][:].rearrange("q (p t) -> q p t", t=PACK),
                                  in_=turned[k][:].rearrange("q t p -> q p t"), func=COPY, scale=DZ_SCALE)
 
-        def round_pass1(t):
-            c = slice(P * t, P * (t + 1))
-            nc.vector.tensor_scalar(out=slots_last(grouped["dz1"][:, c, :]), in0=slots_first(s_pass1[:, :, c]),
+        def round_upper(g, t0, t1):
+            nc.vector.tensor_scalar(out=slots_last(grouped[f"dz{g}"][:, P * t0:P * t1, :]),
+                                    in0=slots_first(s_upper[g][:, :, P * (t0 - LOWER[g]):P * (t1 - LOWER[g])]),
                                     scalar1=DZ_SCALE, scalar2=None, op0=OP.mult)
 
         def turn_back(k):
-            if k == 0:
-                for u in range(2):
-                    back[u] = bank(BACK_BANKS[u], [P, PACK, P])
-            words = dzt[k][:].bitcast(F32)
-            for u in range(2):
-                nc.tensor.transpose(back[u][:, k, :], words[:, u:2 * P:2], ident[:])
+            g = k // PACK
+            for u in range(LOWER[g] // 2):
+                if k % PACK == 0:
+                    back[g, u] = bank(BACK_BANKS[g][u], [P, PACK, P])
+                nc.tensor.transpose(back[g, u][:, k % PACK, :], dzt[k][:].bitcast(F32)[:, u:2 * P:2], ident[:])
 
-        def copy_back(t):
-            halves = back[t // 2][:].rearrange("p j q -> p (j q)").bitcast(BF16).rearrange("p (j q e) -> p e q j", j=PACK, e=2)
-            on_scalar(grouped["dz0"][:, P * t:P * (t + 1), :], halves[:, t % 2, :, :])
+        def copy_back(copy, g, t):
+            halves = back[g, t // 2][:].rearrange("p j q -> p (j q)").bitcast(BF16).rearrange("p (j q e) -> p e q j", j=PACK, e=2)
+            copy(grouped[f"dz{g}"][:, P * t:P * (t + 1), :], halves[:, t % 2, :, :])
+
+        def round_upper_scalar(g, t0, t1):
+            nc.scalar.activation(out=slots_last(grouped[f"dz{g}"][:, P * t0:P * t1, :]),
+                                 in_=slots_first(s_upper[g][:, :, P * (t0 - LOWER[g]):P * (t1 - LOWER[g])]),
+                                 func=COPY, scale=DZ_SCALE)
 
         def times_Eg1(k, out):
             nc.tensor.matmul_mx(out=out, lhsT=dzt_codes[k][:].bitcast(E5M2), lhsT_scale=dzt_scales[k][:],
                                 rhs=codes["Eg1"][:].bitcast(E4M3), rhs_scale=scales["Eg1"][:], start=True, stop=True)
 
-        def out0_product(k):
+        def quantize_unit(k):
             nc.vector.quantize_mx(out=dzt_codes[k][:].bitcast(E5M2), scales=dzt_scales[k][:], in_=dzt[k][:])
+
+        def out0_product(k):
             out0_ps[k] = bank(OUT0_BANKS[k % 2], [P, N])
             times_Eg1(k, out0_ps[k][:])
 
-        def out0_copy(k):
-            on_scalar(out0_sb[k // 2][:, k % 2, :], out0_ps[k][:])
+        def out0_copy(k, copy=on_scalar):
+            copy(out0_sb[k // 2][:, k % 2, :], out0_ps[k][:])
 
         def out0_store(k, n):
             nc.sync.dma_start(out=out0_hbm[k // PACK][:, k % PACK:k % PACK + n, :], in_=out0_sb[k // 2][:, k % 2:k % 2 + n, :])
@@ -172,106 +175,162 @@ def tile_bspncn_pb_v_kernel(tc, e_gen2, e_disc2, e_gen1, e_disc3, j2, v2, x2, Eg
             nc.tensor.matmul_mx(out=out1_ps[t][:], lhsT=codes[f"dz{g}"][:, c].bitcast(E5M2), lhsT_scale=scales[f"dz{g}"][:, c],
                                 rhs=codes[f"e{g}"][:].bitcast(E4M3), rhs_scale=scales[f"e{g}"][:], start=(g == 0), stop=(g == 1))
 
-        def out1_pass0(t):
-            quantize("dz0", P * t, P * (t + 2))
-            out1_product(0, t)
-            out1_product(0, t + 1)
-
-        def out1_pass1(t):
-            quantize("dz1", P * t, P * (t + 1))
-            out1_product(1, t)
-
         def out1_copy(copy, t):
             copy(out1_sb[t // 2][:, t % 2, :], out1_ps[t][:])
 
-        def out1_store(t):
-            nc.sync.dma_start(out=out1_hbm[:, t:t + 2, :], in_=out1_sb[t // 2][:])
+        def out1_store(t, n):
+            nc.sync.dma_start(out=out1_hbm[:, t:t + n, :], in_=out1_sb[t // 2][:, t % 2:t % 2 + n, :])
 
-        def warm_up_plain(name):
+        def warm_up_mx(k, n):
             idle = bank(WARM_BANK, [P, N])
-            nc.tensor.matmul(idle[:], lhsT=ident_gj[:], rhs=loaded[name][:, 0, :], start=True, stop=True)
+            nc.tensor.matmul_mx(out=idle[:, 0:n], lhsT=dzt_codes[k][:].bitcast(E5M2), lhsT_scale=dzt_scales[k][:],
+                                rhs=codes["Eg1"][:, 0:n].bitcast(E4M3), rhs_scale=scales["Eg1"][:, 0:n], start=True, stop=True)
 
-        def warm_up_mx(k):
+        def warm_up(n):
             idle = bank(WARM_BANK, [P, N])
-            times_Eg1(k, idle[:])
+            nc.tensor.matmul(idle[:, 0:n], lhsT=ident_gj[:], rhs=loaded["Eg1"][:, 0, 0:n], start=True, stop=True)
 
         make_identity(nc, ident[:])
         with tc.manual_schedule():
-            load_operand("Eg1")
             load_unit(0)
+            load_operand("Eg1")
             load_operand("e0")
-            for k in range(1, UNITS):
-                load_unit(k)
+            load_unit(1)
+            load_unit(2)
+            load_unit(3)
+            load_unit(4)
+            load_unit(5)
+            load_unit(6)
+            load_unit(7)
             load_operand("e1")
             nc.scalar.activation(out=ident_gj[:], in_=ident[:], func=COPY, scale=GJ_WEIGHT)
-
-            interleave_shared("Eg1")
-            warm_up_plain("Eg1")
             turn_gj(0)
+            interleave(on_scalar, "Eg1", 320, 512)
             mask(0)
             turn_kept(0)
-            warm_up_plain("e0")
-            turn_gj(1)
-            quantize("Eg1")
-            interleave_shared("e0")
+            add_upper(0)
+            turn_upper(0)
             round_turned(0)
-            mask(1)
-            turn_kept(1)
-            turn_gj(2)
-            quantize("e0")
+            interleave(on_vector, "Eg1", 0, 320)
+            turn_gj(1)
+            interleave(on_scalar, "e0", 0, 320)
+            quantize("Eg1", 0, 256)
+            warm_up(512)
+            quantize("Eg1", 256, 512)
+            quantize_unit(0)
             out0_product(0)
-            turn_back(0)
+            out0_copy(0, on_scalar)
+            mask(1)
+            warm_up(512)
+            interleave(on_scalar, "e0", 320, 384)
+            interleave(on_vector, "e0", 384, 512)
+            turn_kept(1)
+            add_upper(1)
+            turn_upper(1)
             round_turned(1)
-            out0_copy(0)
             mask(2)
-            turn_kept(2)
-            turn_gj(3)
-            out0_product(1)
-            round_turned(2)
-            out0_copy(1)
-            out0_store(0, 2)
+            turn_back(0)
+            quantize("e0", 0, 256)
+            turn_gj(2)
+            add_upper(2)
+            warm_up_mx(0, 512)
             mask(3)
-            turn_kept(3)
+            turn_kept(2)
+            quantize_unit(1)
+            turn_upper(2)
+            round_turned(2)
+            quantize("e0", 256, 512)
             turn_back(1)
-            turn_back(2)
+            add_upper(3)
+            turn_gj(3)
+            mask(4)
+            out0_product(1)
+            out0_copy(1, on_scalar)
+            quantize_unit(2)
+            out0_store(0, 2)
+            turn_kept(3)
+            round_upper(0, 2, 3)
+            turn_upper(3)
             round_turned(3)
-
-            for k in range(PACK, UNITS):
-                mask(k)
-                out0_product(k - 2)
-                add_on_vector(k)
-                warm_up_mx(k - 2)
-                turn_sum(k)
-                if k == PACK:
-                    turn_back(PACK - 1)
-                elif k < UNITS - 1:
-                    copy_back(k - PACK - 1)
-                out0_copy(k - 2)
-                if k % 2 == 1:
-                    out0_store(k - 3, 2)
-                round_turned(k)
-
-            interleave(on_vector, "e1", 0, N)
-            out0_product(UNITS - 2)
-            out1_pass0(0)
-            quantize("e1")
-            out0_product(UNITS - 1)
-            for i in range(2):
-                copy_back(2 + i)
-                out0_copy(UNITS - 2 + i)
-                out0_store(UNITS - 2 + i, 1)
-            round_pass1(0)
-            round_pass1(1)
-            out1_pass1(0)
-            out1_pass1(1)
-            out1_copy(on_scalar, 0)
-            out1_copy(on_scalar, 1)
-            out1_store(0)
-            round_pass1(2)
-            out1_pass0(2)
-            round_pass1(3)
-            out1_pass1(2)
-            out1_pass1(3)
-            out1_copy(on_vector, 2)
+            add_upper(4)
+            turn_back(2)
+            mask(5)
+            turn_gj(4)
+            quantize_unit(3)
+            out0_product(2)
+            out0_copy(2, on_scalar)
+            round_upper(0, 3, 4)
+            turn_kept(4)
+            add_upper(5)
+            turn_upper(4)
+            round_turned(4)
+            mask(6)
+            turn_back(3)
+            copy_back(on_scalar, 0, 0)
+            quantize_unit(4)
+            turn_gj(5)
+            quantize("dz0", 256, 512)
+            out0_product(3)
+            out0_copy(3, on_scalar)
+            add_upper(6)
+            out0_store(2, 2)
+            turn_kept(5)
+            mask(7)
+            turn_upper(5)
+            round_turned(5)
+            quantize_unit(5)
+            turn_back(4)
+            add_upper(7)
+            turn_gj(6)
+            interleave(on_vector, "e1", 0, 256)
+            out0_product(4)
+            out0_copy(4, on_scalar)
+            out1_product(0, 2)
+            turn_kept(6)
+            turn_upper(6)
+            round_turned(6)
+            quantize_unit(6)
+            turn_back(5)
+            interleave(on_vector, "e1", 256, 512)
+            turn_gj(7)
+            round_upper(1, 2, 3)
+            out0_product(5)
+            out0_copy(5, on_scalar)
+            out0_store(4, 2)
+            turn_kept(7)
+            turn_upper(7)
+            round_turned(7)
+            quantize_unit(7)
+            turn_back(6)
+            copy_back(on_scalar, 0, 1)
+            quantize("e1", 0, 512)
+            out1_product(0, 3)
+            quantize("dz1", 256, 384)
+            out0_product(6)
+            out0_copy(6, on_scalar)
+            round_upper(1, 3, 4)
+            out0_store(6, 1)
+            turn_back(7)
+            copy_back(on_scalar, 1, 0)
+            quantize("dz0", 0, 256)
+            out0_product(7)
+            out0_copy(7, on_scalar)
+            quantize("dz1", 384, 512)
+            out0_store(7, 1)
+            out1_product(1, 2)
+            copy_back(on_scalar, 1, 1)
+            quantize("dz1", 0, 128)
+            out1_product(1, 3)
             out1_copy(on_scalar, 3)
-            out1_store(2)
+            out1_copy(on_vector, 2)
+            out1_store(2, 1)
+            out1_store(3, 1)
+            out1_product(0, 0)
+            quantize("dz1", 128, 256)
+            out1_product(1, 0)
+            out1_copy(on_vector, 0)
+            out1_store(0, 1)
+            out1_product(0, 1)
+            out1_product(1, 1)
+            out1_copy(on_scalar, 1)
+            out1_store(1, 1)

@@ -57,7 +57,8 @@ def tile_bspncn_pb_v_kernel(tc, e_gen2, e_disc2, e_gen1, e_disc3, j2, v2, x2, Eg
         ident_gj = sb("ident_gj", [P, P], BF16)
         v_pre_sb = [sb(f"v{k}", [P, N], F32) for k in range(UNITS)]
         grad_sb = [sb(f"grad{k}", [P, 2 * N], BF16) for k in range(UNITS)]
-        kept = [sb(f"kept{k}", [P, N], F32) for k in range(UNITS)]
+        kept_lower = [sb(f"kept_lower{k}", [P, 2, P], F32) for k in range(UNITS)]
+        kept_upper = [sb(f"kept_upper{k}", [P, P, 2], BF16) for k in range(UNITS)]
         s_upper = [sb(f"s_upper{g}", [P, PACK, N - P * LOWER[g]], F32) if LOWER[g] < PACK else None for g in range(2)]
         loaded = {name: sb(f"loaded_{name}", [P, PACK, N], BF16) for name in operand_hbm}
         wide = ("Eg1", "e0", "e1", "dz0", "dz1")
@@ -98,16 +99,20 @@ def tile_bspncn_pb_v_kernel(tc, e_gen2, e_disc2, e_gen1, e_disc3, j2, v2, x2, Eg
             nc.vector.quantize_mx(out=codes[name][:, c0:c1].bitcast(fmt), scales=scales[name][:, c0:c1],
                                   in_=grouped[name][:, c0:c1, :].rearrange("p c j -> p (c j)"))
 
-        def mask(k):
-            v, gv = (ap.rearrange("p (q t) -> p q t", t=PACK) for ap in (v_pre_sb[k][:], grad_sb[k][:, N:2 * N]))
-            nc.vector.scalar_tensor_tensor(out=kept[k][:].rearrange("p (t q) -> p q t", t=PACK), in0=v, scalar=THRESHOLD,
-                                           in1=gv, op0=OP.is_lt, op1=OP.mult)
+        def mask(k, out, t):
+            v, gv = (ap.rearrange("p (q t) -> p q t", t=PACK)[:, :, t:t + 2] for ap in (v_pre_sb[k][:], grad_sb[k][:, N:2 * N]))
+            nc.vector.scalar_tensor_tensor(out=out, in0=v, scalar=THRESHOLD, in1=gv, op0=OP.is_lt, op1=OP.mult)
+
+        def mask_lower(k):
+            mask(k, kept_lower[k][:].rearrange("p t q -> p q t"), 0)
+
+        def mask_upper(k):
+            mask(k, kept_upper[k][:], 2)
 
         def add_upper(k):
-            low = LOWER[k // PACK]
-            gj = grad_sb[k][:, 0:N].rearrange("p (q t) -> p t q", t=PACK)[:, low:PACK, :]
+            gj = grad_sb[k][:, 0:N].rearrange("p (q t) -> p t q", t=PACK)[:, 2:PACK, :]
             nc.vector.scalar_tensor_tensor(out=s_upper[k // PACK][:, k % PACK, :].rearrange("p (t q) -> p t q", q=P), in0=gj,
-                                           scalar=GJ_WEIGHT, in1=kept[k][:, P * low:N].rearrange("p (t q) -> p t q", q=P),
+                                           scalar=GJ_WEIGHT, in1=kept_upper[k][:].rearrange("p q t -> p t q"),
                                            op0=OP.mult, op1=OP.add)
 
         def turn_gj(k):
@@ -118,7 +123,7 @@ def tile_bspncn_pb_v_kernel(tc, e_gen2, e_disc2, e_gen1, e_disc3, j2, v2, x2, Eg
         def turn_kept(k):
             low = LOWER[k // PACK]
             for t in range(low):
-                nc.tensor.matmul(turned[k][:, t, :], lhsT=kept[k][:, P * t:P * (t + 1)], rhs=ident[:], is_transpose=True,
+                nc.tensor.matmul(turned[k][:, t, :], lhsT=kept_lower[k][:, t, :], rhs=ident[:], is_transpose=True,
                                  start=False, stop=(t == low - 1))
 
         def turn_upper(k):
@@ -206,7 +211,8 @@ def tile_bspncn_pb_v_kernel(tc, e_gen2, e_disc2, e_gen1, e_disc3, j2, v2, x2, Eg
             nc.scalar.activation(out=ident_gj[:], in_=ident[:], func=COPY, scale=GJ_WEIGHT)
             turn_gj(0)
             interleave(on_scalar, "Eg1", 320, 512)
-            mask(0)
+            mask_upper(0)
+            mask_lower(0)
             turn_kept(0)
             add_upper(0)
             turn_upper(0)
@@ -220,91 +226,98 @@ def tile_bspncn_pb_v_kernel(tc, e_gen2, e_disc2, e_gen1, e_disc3, j2, v2, x2, Eg
             quantize_unit(0)
             out0_product(0)
             out0_copy(0, on_scalar)
-            mask(1)
-            warm_up(512)
+            mask_upper(1)
             interleave(on_scalar, "e0", 320, 384)
-            interleave(on_vector, "e0", 384, 512)
+            mask_lower(1)
             turn_kept(1)
             add_upper(1)
             turn_upper(1)
             round_turned(1)
-            mask(2)
+            mask_upper(2)
+            warm_up(512)
+            interleave(on_scalar, "e0", 384, 512)
+            mask_lower(2)
             turn_back(0)
-            quantize("e0", 0, 256)
-            turn_gj(2)
             add_upper(2)
-            warm_up_mx(0, 512)
-            mask(3)
+            turn_gj(2)
+            quantize("e0", 0, 256)
             turn_kept(2)
-            quantize_unit(1)
+            mask_upper(3)
             turn_upper(2)
             round_turned(2)
-            quantize("e0", 256, 512)
+            quantize_unit(1)
+            warm_up_mx(0, 512)
+            mask_lower(3)
             turn_back(1)
             add_upper(3)
             turn_gj(3)
-            mask(4)
+            mask_upper(4)
             out0_product(1)
             out0_copy(1, on_scalar)
-            quantize_unit(2)
+            mask_lower(4)
             out0_store(0, 2)
             turn_kept(3)
-            round_upper(0, 2, 3)
+            add_upper(4)
             turn_upper(3)
             round_turned(3)
-            add_upper(4)
-            turn_back(2)
-            mask(5)
+            quantize_unit(2)
             turn_gj(4)
-            quantize_unit(3)
-            out0_product(2)
-            out0_copy(2, on_scalar)
-            round_upper(0, 3, 4)
+            round_upper_scalar(0, 2, 3)
+            quantize("e0", 256, 512)
             turn_kept(4)
-            add_upper(5)
+            mask_upper(5)
             turn_upper(4)
             round_turned(4)
-            mask(6)
-            turn_back(3)
-            copy_back(on_scalar, 0, 0)
-            quantize_unit(4)
+            mask_lower(5)
+            turn_back(2)
+            add_upper(5)
+            out0_product(2)
+            out0_copy(2, on_scalar)
+            quantize_unit(3)
             turn_gj(5)
-            quantize("dz0", 256, 512)
-            out0_product(3)
-            out0_copy(3, on_scalar)
-            add_upper(6)
-            out0_store(2, 2)
+            round_upper(0, 3, 4)
             turn_kept(5)
-            mask(7)
+            mask_upper(6)
             turn_upper(5)
             round_turned(5)
-            quantize_unit(5)
-            turn_back(4)
-            add_upper(7)
+            mask_lower(6)
+            turn_back(3)
+            add_upper(6)
+            out0_product(3)
+            out0_copy(3, on_scalar)
+            quantize_unit(4)
+            out0_store(2, 2)
             turn_gj(6)
-            interleave(on_vector, "e1", 0, 256)
-            out0_product(4)
-            out0_copy(4, on_scalar)
-            out1_product(0, 2)
+            quantize("dz0", 256, 512)
             turn_kept(6)
+            mask_upper(7)
             turn_upper(6)
             round_turned(6)
-            quantize_unit(6)
-            turn_back(5)
-            interleave(on_vector, "e1", 256, 512)
+            mask_lower(7)
+            turn_back(4)
+            add_upper(7)
+            out0_product(4)
+            out0_copy(4, on_scalar)
+            quantize_unit(5)
+            out1_product(0, 2)
+            copy_back(on_vector, 0, 0)
             turn_gj(7)
+            interleave(on_vector, "e1", 0, 256)
+            turn_kept(7)
+            quantize_unit(6)
+            turn_upper(7)
+            round_turned(7)
+            interleave(on_vector, "e1", 256, 512)
+            turn_back(5)
             round_upper(1, 2, 3)
             out0_product(5)
             out0_copy(5, on_scalar)
-            out0_store(4, 2)
-            turn_kept(7)
-            turn_upper(7)
-            round_turned(7)
             quantize_unit(7)
-            turn_back(6)
+            out0_store(4, 2)
+            out1_product(0, 3)
             copy_back(on_scalar, 0, 1)
             quantize("e1", 0, 512)
-            out1_product(0, 3)
+            turn_back(6)
             quantize("dz1", 256, 384)
             out0_product(6)
             out0_copy(6, on_scalar)

@@ -28,6 +28,8 @@ BACK_BANKS = ((2,), (3,))
 OUT0_BANKS = (4,5)
 OUT1_BANKS = (2,0,6,7)
 WARM_BANK = 7
+GRAD_LOADS = ((0, 1), (1, 1), (2, 1), (3, 1), (4, 1), (5, 1), (6, 1), (7, 1))
+V_LOADS = ((0, 1), (1, 1), (2, 1), (3, 1), (4, 1), (5, 1), (6, 1), (7, 1))
 
 FLOPS = 2 * 2 * SAMPLES * N * N
 BYTES = SAMPLES * N * (4 + 2 + 2 + 2) + N * N * 2 + SAMPLES * N * 4 + N * N * 4
@@ -55,8 +57,10 @@ def tile_bspncn_pb_v_kernel(tc, e_gen2, e_disc2, e_gen1, e_disc3, j2, v2, x2, Eg
 
         ident = sb("ident", [P, P], F32)
         ident_gj = sb("ident_gj", [P, P], BF16)
-        v_pre_sb = [sb(f"v{k}", [P, N], F32) for k in range(UNITS)]
-        grad_sb = [sb(f"grad{k}", [P, 2 * N], BF16) for k in range(UNITS)]
+        v_tiles = {k: sb(f"v{k}", [P, n, N], F32) for k, n in V_LOADS}
+        grad_tiles = {k: sb(f"grad{k}", [P, n, 2 * N], BF16) for k, n in GRAD_LOADS}
+        v_pre_sb = [v_tiles[k][:, i, :] for k, n in V_LOADS for i in range(n)]
+        grad_sb = [grad_tiles[k][:, i, :] for k, n in GRAD_LOADS for i in range(n)]
         kept_lower = [sb(f"kept_lower{k}", [P, 2, P], F32) for k in range(UNITS)]
         kept_upper = [sb(f"kept_upper{k}", [P, P, 2], BF16) for k in range(UNITS)]
         s_upper = [sb(f"s_upper{g}", [P, PACK, N - P * LOWER[g]], F32) if LOWER[g] < PACK else None for g in range(2)]
@@ -68,13 +72,15 @@ def tile_bspncn_pb_v_kernel(tc, e_gen2, e_disc2, e_gen1, e_disc3, j2, v2, x2, Eg
         dzt = [sb(f"dzt{k}", [P, P * PACK], BF16) for k in range(UNITS)]
         dzt_codes = [sb(f"dzt_codes{k}", [P, P], U32) for k in range(UNITS)]
         dzt_scales = [sb(f"dzt_scales{k}", [P, P], U8) for k in range(UNITS)]
-        out0_sb = [sb(f"out0_{i}", [P, 2, N], F32) for i in range(UNITS // 2)]
+        out0_sb = [sb(f"out0_{g}", [P, PACK, N], F32) for g in range(2)]
         out1_sb = [sb(f"out1_{i}", [P, 2, N], F32) for i in range(PACK // 2)]
-        turned, back, out0_ps, out1_ps = {}, {}, {}, {}
+        turned, back, out0_ps, out1_ps, last_ps = {}, {}, {}, {}, {}
 
-        def load_unit(k):
-            nc.sync.dma_start(out=grad_sb[k][:], in_=grad_hbm[k // PACK][:, k % PACK, 0:2 * N])
-            nc.sync.dma_start(out=v_pre_sb[k][:], in_=v_hbm[k // PACK][:, k % PACK, :])
+        def load_grad(k, n):
+            nc.sync.dma_start(out=grad_tiles[k][:], in_=grad_hbm[k // PACK][:, k % PACK:k % PACK + n, 0:2 * N])
+
+        def load_v(k, n):
+            nc.sync.dma_start(out=v_tiles[k][:], in_=v_hbm[k // PACK][:, k % PACK:k % PACK + n, :])
 
         def load_operand(name):
             nc.sync.dma_start(out=loaded[name][:], in_=operand_hbm[name])
@@ -100,7 +106,7 @@ def tile_bspncn_pb_v_kernel(tc, e_gen2, e_disc2, e_gen1, e_disc3, j2, v2, x2, Eg
                                   in_=grouped[name][:, c0:c1, :].rearrange("p c j -> p (c j)"))
 
         def mask(k, out, t):
-            v, gv = (ap.rearrange("p (q t) -> p q t", t=PACK)[:, :, t:t + 2] for ap in (v_pre_sb[k][:], grad_sb[k][:, N:2 * N]))
+            v, gv = (ap.rearrange("p (q t) -> p q t", t=PACK)[:, :, t:t + 2] for ap in (v_pre_sb[k], grad_sb[k][:, N:2 * N]))
             nc.vector.scalar_tensor_tensor(out=out, in0=v, scalar=THRESHOLD, in1=gv, op0=OP.is_lt, op1=OP.mult)
 
         def mask_lower(k):
@@ -168,10 +174,10 @@ def tile_bspncn_pb_v_kernel(tc, e_gen2, e_disc2, e_gen1, e_disc3, j2, v2, x2, Eg
             times_Eg1(k, out0_ps[k][:])
 
         def out0_copy(k, copy=on_scalar):
-            copy(out0_sb[k // 2][:, k % 2, :], out0_ps[k][:])
+            copy(out0_sb[k // PACK][:, k % PACK, :], out0_ps[k][:])
 
         def out0_store(k, n):
-            nc.sync.dma_start(out=out0_hbm[k // PACK][:, k % PACK:k % PACK + n, :], in_=out0_sb[k // 2][:, k % 2:k % 2 + n, :])
+            nc.sync.dma_start(out=out0_hbm[k // PACK][:, k % PACK:k % PACK + n, :], in_=out0_sb[k // PACK][:, k % PACK:k % PACK + n, :])
 
         def out1_product(g, t):
             if g == 0:
@@ -182,6 +188,17 @@ def tile_bspncn_pb_v_kernel(tc, e_gen2, e_disc2, e_gen1, e_disc3, j2, v2, x2, Eg
 
         def out1_copy(copy, t):
             copy(out1_sb[t // 2][:, t % 2, :], out1_ps[t][:])
+
+        def last_product(g, h):
+            if g == 0:
+                last_ps[h] = bank(TURN_BANKS[h], [P, HALF])
+            c = slice(P, 2 * P)
+            n = slice(HALF * h, HALF * (h + 1))
+            nc.tensor.matmul_mx(out=last_ps[h][:], lhsT=codes[f"dz{g}"][:, c].bitcast(E5M2), lhsT_scale=scales[f"dz{g}"][:, c],
+                                rhs=codes[f"e{g}"][:, n].bitcast(E4M3), rhs_scale=scales[f"e{g}"][:, n], start=(g == 0), stop=(g == 1))
+
+        def last_copy(copy, h):
+            copy(out1_sb[0][:, 1, HALF * h:HALF * (h + 1)], last_ps[h][:])
 
         def out1_store(t, n):
             nc.sync.dma_start(out=out1_hbm[:, t:t + n, :], in_=out1_sb[t // 2][:, t % 2:t % 2 + n, :])
@@ -197,16 +214,24 @@ def tile_bspncn_pb_v_kernel(tc, e_gen2, e_disc2, e_gen1, e_disc3, j2, v2, x2, Eg
 
         make_identity(nc, ident[:])
         with tc.manual_schedule():
-            load_unit(0)
+            load_grad(0, 1)
+            load_v(0, 1)
             load_operand("Eg1")
             load_operand("e0")
-            load_unit(1)
-            load_unit(2)
-            load_unit(3)
-            load_unit(4)
-            load_unit(5)
-            load_unit(6)
-            load_unit(7)
+            load_grad(1, 1)
+            load_v(1, 1)
+            load_grad(2, 1)
+            load_v(2, 1)
+            load_grad(3, 1)
+            load_v(3, 1)
+            load_grad(4, 1)
+            load_v(4, 1)
+            load_grad(5, 1)
+            load_v(5, 1)
+            load_grad(6, 1)
+            load_v(6, 1)
+            load_grad(7, 1)
+            load_v(7, 1)
             load_operand("e1")
             nc.scalar.activation(out=ident_gj[:], in_=ident[:], func=COPY, scale=GJ_WEIGHT)
             turn_gj(0)
@@ -245,24 +270,24 @@ def tile_bspncn_pb_v_kernel(tc, e_gen2, e_disc2, e_gen1, e_disc3, j2, v2, x2, Eg
             mask_upper(3)
             turn_upper(2)
             round_turned(2)
-            quantize_unit(1)
-            warm_up_mx(0, 512)
             mask_lower(3)
-            turn_back(1)
+            warm_up_mx(0, 512)
             add_upper(3)
             turn_gj(3)
-            mask_upper(4)
-            out0_product(1)
-            out0_copy(1, on_scalar)
-            mask_lower(4)
-            out0_store(0, 2)
+            round_upper_scalar(0, 2, 3)
+            quantize_unit(1)
             turn_kept(3)
-            add_upper(4)
+            mask_upper(4)
             turn_upper(3)
             round_turned(3)
+            mask_lower(4)
+            turn_back(1)
+            add_upper(4)
+            out0_product(1)
+            out0_copy(1, on_scalar)
             quantize_unit(2)
+            out0_store(0, 2)
             turn_gj(4)
-            round_upper_scalar(0, 2, 3)
             quantize("e0", 256, 512)
             turn_kept(4)
             mask_upper(5)
@@ -275,7 +300,8 @@ def tile_bspncn_pb_v_kernel(tc, e_gen2, e_disc2, e_gen1, e_disc3, j2, v2, x2, Eg
             out0_copy(2, on_scalar)
             quantize_unit(3)
             turn_gj(5)
-            round_upper(0, 3, 4)
+            round_upper_scalar(0, 3, 4)
+            quantize("dz0", 256, 384)
             turn_kept(5)
             mask_upper(6)
             turn_upper(5)
@@ -287,19 +313,19 @@ def tile_bspncn_pb_v_kernel(tc, e_gen2, e_disc2, e_gen1, e_disc3, j2, v2, x2, Eg
             out0_copy(3, on_scalar)
             quantize_unit(4)
             out0_store(2, 2)
-            turn_gj(6)
-            quantize("dz0", 256, 512)
-            turn_kept(6)
+            out1_product(0, 2)
             mask_upper(7)
+            turn_gj(6)
+            mask_lower(7)
+            turn_kept(6)
+            add_upper(7)
             turn_upper(6)
             round_turned(6)
-            mask_lower(7)
+            quantize_unit(5)
             turn_back(4)
-            add_upper(7)
+            quantize("dz0", 384, 512)
             out0_product(4)
             out0_copy(4, on_scalar)
-            quantize_unit(5)
-            out1_product(0, 2)
             copy_back(on_vector, 0, 0)
             turn_gj(7)
             interleave(on_vector, "e1", 0, 256)
@@ -343,7 +369,10 @@ def tile_bspncn_pb_v_kernel(tc, e_gen2, e_disc2, e_gen1, e_disc3, j2, v2, x2, Eg
             out1_product(1, 0)
             out1_copy(on_vector, 0)
             out1_store(0, 1)
-            out1_product(0, 1)
-            out1_product(1, 1)
-            out1_copy(on_scalar, 1)
+            last_product(0, 0)
+            last_product(0, 1)
+            last_product(1, 1)
+            last_copy(on_scalar, 1)
+            last_product(1, 0)
+            last_copy(on_vector, 0)
             out1_store(1, 1)

@@ -15,21 +15,25 @@ COPY = mybir.ActivationFunctionType.Copy
 P = 128
 PACK = 4
 N = 512
+HALF = N // 2
 SAMPLES = 1024
 UNITS = SAMPLES // P
-HALF = N // 2
+LOWER = (0, 1)
+UPPER = (2, 3)
 THRESHOLD = 0.4
 GJ_WEIGHT = 20.0
 DZ_SCALE = 0.005
+LAG = 2
 
-LOWER = (2,2)
-TURN_BANKS = (0,1,0,1,0,1,0,1)
-BACK_BANKS = ((2,), (3,))
-OUT0_BANKS = (4,5)
-OUT1_BANKS = (2,0,6,7)
+EG1_ON_VECTOR = 320
+E0_CUTS = (0, 320, 384, N)
+
+TURN_BANKS = (0, 1)
+BACK_BANKS = (2, 3)
+OUT0_BANKS = (4, 5)
+OUT1_BANKS = {0: 2, 2: 6, 3: 7}
 WARM_BANK = 7
-GRAD_LOADS = ((0, 1), (1, 1), (2, 1), (3, 1), (4, 1), (5, 1), (6, 1), (7, 1))
-V_LOADS = ((0, 1), (1, 1), (2, 1), (3, 1), (4, 1), (5, 1), (6, 1), (7, 1))
+LAST_TILE = 1
 
 FLOPS = 2 * 2 * SAMPLES * N * N
 BYTES = SAMPLES * N * (4 + 2 + 2 + 2) + N * N * 2 + SAMPLES * N * 4 + N * N * 4
@@ -57,13 +61,11 @@ def tile_bspncn_pb_v_kernel(tc, e_gen2, e_disc2, e_gen1, e_disc3, j2, v2, x2, Eg
 
         ident = sb("ident", [P, P], F32)
         ident_gj = sb("ident_gj", [P, P], BF16)
-        v_tiles = {k: sb(f"v{k}", [P, n, N], F32) for k, n in V_LOADS}
-        grad_tiles = {k: sb(f"grad{k}", [P, n, 2 * N], BF16) for k, n in GRAD_LOADS}
-        v_pre_sb = [v_tiles[k][:, i, :] for k, n in V_LOADS for i in range(n)]
-        grad_sb = [grad_tiles[k][:, i, :] for k, n in GRAD_LOADS for i in range(n)]
+        v_pre_sb = [sb(f"v{k}", [P, N], F32) for k in range(UNITS)]
+        grad_sb = [sb(f"grad{k}", [P, 2 * N], BF16) for k in range(UNITS)]
         kept_lower = [sb(f"kept_lower{k}", [P, 2, P], F32) for k in range(UNITS)]
         kept_upper = [sb(f"kept_upper{k}", [P, P, 2], BF16) for k in range(UNITS)]
-        s_upper = [sb(f"s_upper{g}", [P, PACK, N - P * LOWER[g]], F32) if LOWER[g] < PACK else None for g in range(2)]
+        s_upper = [sb(f"s_upper{g}", [P, PACK, HALF], F32) for g in range(2)]
         loaded = {name: sb(f"loaded_{name}", [P, PACK, N], BF16) for name in operand_hbm}
         wide = ("Eg1", "e0", "e1", "dz0", "dz1")
         grouped = {name: sb(f"grouped_{name}", [P, N, PACK], BF16) for name in wide}
@@ -73,14 +75,12 @@ def tile_bspncn_pb_v_kernel(tc, e_gen2, e_disc2, e_gen1, e_disc3, j2, v2, x2, Eg
         dzt_codes = [sb(f"dzt_codes{k}", [P, P], U32) for k in range(UNITS)]
         dzt_scales = [sb(f"dzt_scales{k}", [P, P], U8) for k in range(UNITS)]
         out0_sb = [sb(f"out0_{g}", [P, PACK, N], F32) for g in range(2)]
-        out1_sb = [sb(f"out1_{i}", [P, 2, N], F32) for i in range(PACK // 2)]
+        out1_sb = [sb(f"out1_{t}", [P, N], F32) for t in range(PACK)]
         turned, back, out0_ps, out1_ps, last_ps = {}, {}, {}, {}, {}
 
-        def load_grad(k, n):
-            nc.sync.dma_start(out=grad_tiles[k][:], in_=grad_hbm[k // PACK][:, k % PACK:k % PACK + n, 0:2 * N])
-
-        def load_v(k, n):
-            nc.sync.dma_start(out=v_tiles[k][:], in_=v_hbm[k // PACK][:, k % PACK:k % PACK + n, :])
+        def load_unit(k):
+            nc.sync.dma_start(out=grad_sb[k][:], in_=grad_hbm[k // PACK][:, k % PACK, 0:2 * N])
+            nc.sync.dma_start(out=v_pre_sb[k][:], in_=v_hbm[k // PACK][:, k % PACK, :])
 
         def load_operand(name):
             nc.sync.dma_start(out=loaded[name][:], in_=operand_hbm[name])
@@ -91,6 +91,12 @@ def tile_bspncn_pb_v_kernel(tc, e_gen2, e_disc2, e_gen1, e_disc3, j2, v2, x2, Eg
         def on_scalar(out, in_):
             nc.scalar.copy(out=out, in_=in_)
 
+        def scaled_on_vector(out, in_):
+            nc.vector.tensor_scalar(out=out, in0=in_, scalar1=DZ_SCALE, scalar2=None, op0=OP.mult)
+
+        def scaled_on_scalar(out, in_):
+            nc.scalar.activation(out=out, in_=in_, func=COPY, scale=DZ_SCALE)
+
         def slots_first(ap):
             return ap.rearrange("p j (c i) -> p c j i", i=4)
 
@@ -100,279 +106,207 @@ def tile_bspncn_pb_v_kernel(tc, e_gen2, e_disc2, e_gen1, e_disc3, j2, v2, x2, Eg
         def interleave(copy, name, c0, c1):
             copy(slots_last(grouped[name][:, c0:c1, :]), slots_first(loaded[name][:, :, c0:c1]))
 
-        def quantize(name, c0=0, c1=N):
+        def quantize(name, c0, c1):
             fmt = E5M2 if name.startswith("dz") else E4M3
             nc.vector.quantize_mx(out=codes[name][:, c0:c1].bitcast(fmt), scales=scales[name][:, c0:c1],
                                   in_=grouped[name][:, c0:c1, :].rearrange("p c j -> p (c j)"))
 
-        def mask(k, out, t):
-            v, gv = (ap.rearrange("p (q t) -> p q t", t=PACK)[:, :, t:t + 2] for ap in (v_pre_sb[k], grad_sb[k][:, N:2 * N]))
-            nc.vector.scalar_tensor_tensor(out=out, in0=v, scalar=THRESHOLD, in1=gv, op0=OP.is_lt, op1=OP.mult)
+        def quantize_tile(g, t):
+            quantize(f"dz{g}", P * t, P * (t + 1))
 
-        def mask_lower(k):
-            mask(k, kept_lower[k][:].rearrange("p t q -> p q t"), 0)
+        def by_slot(ap, slots):
+            return ap.rearrange("p (q t) -> p q t", t=PACK)[:, :, slots[0]:slots[1] + 1]
 
-        def mask_upper(k):
-            mask(k, kept_upper[k][:], 2)
+        def mask(k, slots, out):
+            nc.vector.scalar_tensor_tensor(out=out, in0=by_slot(v_pre_sb[k][:], slots), scalar=THRESHOLD,
+                                           in1=by_slot(grad_sb[k][:, N:2 * N], slots), op0=OP.is_lt, op1=OP.mult)
 
-        def add_upper(k):
-            gj = grad_sb[k][:, 0:N].rearrange("p (q t) -> p t q", t=PACK)[:, 2:PACK, :]
-            nc.vector.scalar_tensor_tensor(out=s_upper[k // PACK][:, k % PACK, :].rearrange("p (t q) -> p t q", q=P), in0=gj,
+        def masks_and_sum(k):
+            mask(k, UPPER, kept_upper[k][:])
+            mask(k, LOWER, kept_lower[k][:].rearrange("p t q -> p q t"))
+            nc.vector.scalar_tensor_tensor(out=s_upper[k // PACK][:, k % PACK, :].rearrange("p (t q) -> p t q", q=P),
+                                           in0=by_slot(grad_sb[k][:, 0:N], UPPER).rearrange("p q t -> p t q"),
                                            scalar=GJ_WEIGHT, in1=kept_upper[k][:].rearrange("p q t -> p t q"),
                                            op0=OP.mult, op1=OP.add)
 
         def turn_gj(k):
-            turned[k] = bank(TURN_BANKS[k], [P, PACK, P])
-            for t in range(LOWER[k // PACK]):
-                nc.tensor.matmul(turned[k][:, t, :], lhsT=grad_sb[k][:, t:N:PACK], rhs=ident_gj[:], start=(t == 0), stop=False)
+            turned[k] = bank(TURN_BANKS[k % 2], [P, PACK, P])
+            for t in LOWER:
+                nc.tensor.matmul(turned[k][:, t, :], lhsT=grad_sb[k][:, t:N:PACK], rhs=ident_gj[:],
+                                 start=(t == LOWER[0]), stop=False)
 
-        def turn_kept(k):
-            low = LOWER[k // PACK]
-            for t in range(low):
+        def turn(k):
+            for t in LOWER:
                 nc.tensor.matmul(turned[k][:, t, :], lhsT=kept_lower[k][:, t, :], rhs=ident[:], is_transpose=True,
-                                 start=False, stop=(t == low - 1))
-
-        def turn_upper(k):
-            low = LOWER[k // PACK]
-            for t in range(low, PACK):
-                nc.tensor.transpose(turned[k][:, t, :], s_upper[k // PACK][:, k % PACK, P * (t - low):P * (t - low + 1)], ident[:])
+                                 start=False, stop=(t == LOWER[1]))
+            for i, t in enumerate(UPPER):
+                nc.tensor.transpose(turned[k][:, t, :], s_upper[k // PACK][:, k % PACK, P * i:P * (i + 1)], ident[:])
 
         def round_turned(k):
-            nc.scalar.activation(out=dzt[k][:].rearrange("q (p t) -> q p t", t=PACK),
-                                 in_=turned[k][:].rearrange("q t p -> q p t"), func=COPY, scale=DZ_SCALE)
+            scaled_on_scalar(dzt[k][:].rearrange("q (p t) -> q p t", t=PACK), turned[k][:].rearrange("q t p -> q p t"))
 
-        def round_upper(g, t0, t1):
-            nc.vector.tensor_scalar(out=slots_last(grouped[f"dz{g}"][:, P * t0:P * t1, :]),
-                                    in0=slots_first(s_upper[g][:, :, P * (t0 - LOWER[g]):P * (t1 - LOWER[g])]),
-                                    scalar1=DZ_SCALE, scalar2=None, op0=OP.mult)
+        def round_upper(scaled_copy, g, t):
+            i = t - UPPER[0]
+            scaled_copy(slots_last(grouped[f"dz{g}"][:, P * t:P * (t + 1), :]), slots_first(s_upper[g][:, :, P * i:P * (i + 1)]))
 
         def turn_back(k):
             g = k // PACK
-            for u in range(LOWER[g] // 2):
-                if k % PACK == 0:
-                    back[g, u] = bank(BACK_BANKS[g][u], [P, PACK, P])
-                nc.tensor.transpose(back[g, u][:, k % PACK, :], dzt[k][:].bitcast(F32)[:, u:2 * P:2], ident[:])
+            if k % PACK == 0:
+                back[g] = bank(BACK_BANKS[g], [P, PACK, P])
+            nc.tensor.transpose(back[g][:, k % PACK, :], dzt[k][:].bitcast(F32)[:, 0:2 * P:2], ident[:])
 
         def copy_back(copy, g, t):
-            halves = back[g, t // 2][:].rearrange("p j q -> p (j q)").bitcast(BF16).rearrange("p (j q e) -> p e q j", j=PACK, e=2)
-            copy(grouped[f"dz{g}"][:, P * t:P * (t + 1), :], halves[:, t % 2, :, :])
+            halves = back[g][:].rearrange("p j q -> p (j q)").bitcast(BF16).rearrange("p (j q e) -> p e q j", j=PACK, e=2)
+            copy(grouped[f"dz{g}"][:, P * t:P * (t + 1), :], halves[:, t, :, :])
 
-        def round_upper_scalar(g, t0, t1):
-            nc.scalar.activation(out=slots_last(grouped[f"dz{g}"][:, P * t0:P * t1, :]),
-                                 in_=slots_first(s_upper[g][:, :, P * (t0 - LOWER[g]):P * (t1 - LOWER[g])]),
-                                 func=COPY, scale=DZ_SCALE)
+        def quantize_unit(k):
+            nc.vector.quantize_mx(out=dzt_codes[k][:].bitcast(E5M2), scales=dzt_scales[k][:], in_=dzt[k][:])
 
         def times_Eg1(k, out):
             nc.tensor.matmul_mx(out=out, lhsT=dzt_codes[k][:].bitcast(E5M2), lhsT_scale=dzt_scales[k][:],
                                 rhs=codes["Eg1"][:].bitcast(E4M3), rhs_scale=scales["Eg1"][:], start=True, stop=True)
 
-        def quantize_unit(k):
-            nc.vector.quantize_mx(out=dzt_codes[k][:].bitcast(E5M2), scales=dzt_scales[k][:], in_=dzt[k][:])
-
         def out0_product(k):
             out0_ps[k] = bank(OUT0_BANKS[k % 2], [P, N])
             times_Eg1(k, out0_ps[k][:])
 
-        def out0_copy(k, copy=on_scalar):
-            copy(out0_sb[k // PACK][:, k % PACK, :], out0_ps[k][:])
+        def out0_copy(k):
+            on_scalar(out0_sb[k // PACK][:, k % PACK, :], out0_ps[k][:])
 
         def out0_store(k, n):
-            nc.sync.dma_start(out=out0_hbm[k // PACK][:, k % PACK:k % PACK + n, :], in_=out0_sb[k // PACK][:, k % PACK:k % PACK + n, :])
+            j = slice(k % PACK, k % PACK + n)
+            nc.sync.dma_start(out=out0_hbm[k // PACK][:, j, :], in_=out0_sb[k // PACK][:, j, :])
+
+        def times_e(g, t, n, out):
+            c = slice(P * t, P * (t + 1))
+            nc.tensor.matmul_mx(out=out, lhsT=codes[f"dz{g}"][:, c].bitcast(E5M2), lhsT_scale=scales[f"dz{g}"][:, c],
+                                rhs=codes[f"e{g}"][:, n].bitcast(E4M3), rhs_scale=scales[f"e{g}"][:, n],
+                                start=(g == 0), stop=(g == 1))
 
         def out1_product(g, t):
             if g == 0:
                 out1_ps[t] = bank(OUT1_BANKS[t], [P, N])
-            c = slice(P * t, P * (t + 1))
-            nc.tensor.matmul_mx(out=out1_ps[t][:], lhsT=codes[f"dz{g}"][:, c].bitcast(E5M2), lhsT_scale=scales[f"dz{g}"][:, c],
-                                rhs=codes[f"e{g}"][:].bitcast(E4M3), rhs_scale=scales[f"e{g}"][:], start=(g == 0), stop=(g == 1))
+            times_e(g, t, slice(0, N), out1_ps[t][:])
 
-        def out1_copy(copy, t):
-            copy(out1_sb[t // 2][:, t % 2, :], out1_ps[t][:])
+        def out1_store(t):
+            nc.sync.dma_start(out=out1_hbm[:, t, :], in_=out1_sb[t][:])
+
+        def out1_leave(copy, t):
+            copy(out1_sb[t][:], out1_ps[t][:])
+            out1_store(t)
 
         def last_product(g, h):
             if g == 0:
                 last_ps[h] = bank(TURN_BANKS[h], [P, HALF])
-            c = slice(P, 2 * P)
-            n = slice(HALF * h, HALF * (h + 1))
-            nc.tensor.matmul_mx(out=last_ps[h][:], lhsT=codes[f"dz{g}"][:, c].bitcast(E5M2), lhsT_scale=scales[f"dz{g}"][:, c],
-                                rhs=codes[f"e{g}"][:, n].bitcast(E4M3), rhs_scale=scales[f"e{g}"][:, n], start=(g == 0), stop=(g == 1))
+            times_e(g, LAST_TILE, slice(HALF * h, HALF * (h + 1)), last_ps[h][:])
 
         def last_copy(copy, h):
-            copy(out1_sb[0][:, 1, HALF * h:HALF * (h + 1)], last_ps[h][:])
+            copy(out1_sb[LAST_TILE][:, HALF * h:HALF * (h + 1)], last_ps[h][:])
 
-        def out1_store(t, n):
-            nc.sync.dma_start(out=out1_hbm[:, t:t + n, :], in_=out1_sb[t // 2][:, t % 2:t % 2 + n, :])
-
-        def warm_up_mx(k, n):
+        def warm_up_plain():
             idle = bank(WARM_BANK, [P, N])
-            nc.tensor.matmul_mx(out=idle[:, 0:n], lhsT=dzt_codes[k][:].bitcast(E5M2), lhsT_scale=dzt_scales[k][:],
-                                rhs=codes["Eg1"][:, 0:n].bitcast(E4M3), rhs_scale=scales["Eg1"][:, 0:n], start=True, stop=True)
+            nc.tensor.matmul(idle[:], lhsT=ident_gj[:], rhs=loaded["Eg1"][:, 0, :], start=True, stop=True)
 
-        def warm_up(n):
+        def warm_up_mx():
             idle = bank(WARM_BANK, [P, N])
-            nc.tensor.matmul(idle[:, 0:n], lhsT=ident_gj[:], rhs=loaded["Eg1"][:, 0, 0:n], start=True, stop=True)
+            times_Eg1(0, idle[:])
 
         make_identity(nc, ident[:])
         with tc.manual_schedule():
-            load_grad(0, 1)
-            load_v(0, 1)
+            load_unit(0)
             load_operand("Eg1")
             load_operand("e0")
-            load_grad(1, 1)
-            load_v(1, 1)
-            load_grad(2, 1)
-            load_v(2, 1)
-            load_grad(3, 1)
-            load_v(3, 1)
-            load_grad(4, 1)
-            load_v(4, 1)
-            load_grad(5, 1)
-            load_v(5, 1)
-            load_grad(6, 1)
-            load_v(6, 1)
-            load_grad(7, 1)
-            load_v(7, 1)
+            for k in range(1, UNITS):
+                load_unit(k)
             load_operand("e1")
             nc.scalar.activation(out=ident_gj[:], in_=ident[:], func=COPY, scale=GJ_WEIGHT)
+
             turn_gj(0)
-            interleave(on_scalar, "Eg1", 320, 512)
-            mask_upper(0)
-            mask_lower(0)
-            turn_kept(0)
-            add_upper(0)
-            turn_upper(0)
+            masks_and_sum(0)
+            turn(0)
+            interleave(on_scalar, "Eg1", EG1_ON_VECTOR, N)
+            interleave(on_vector, "Eg1", 0, EG1_ON_VECTOR)
             round_turned(0)
-            interleave(on_vector, "Eg1", 0, 320)
-            turn_gj(1)
-            interleave(on_scalar, "e0", 0, 320)
-            quantize("Eg1", 0, 256)
-            warm_up(512)
-            quantize("Eg1", 256, 512)
+            interleave(on_scalar, "e0", E0_CUTS[0], E0_CUTS[1])
+            quantize("Eg1", 0, HALF)
+            quantize("Eg1", HALF, N)
             quantize_unit(0)
+            turn_gj(1)
+            warm_up_plain()
             out0_product(0)
-            out0_copy(0, on_scalar)
-            mask_upper(1)
-            interleave(on_scalar, "e0", 320, 384)
-            mask_lower(1)
-            turn_kept(1)
-            add_upper(1)
-            turn_upper(1)
-            round_turned(1)
-            mask_upper(2)
-            warm_up(512)
-            interleave(on_scalar, "e0", 384, 512)
-            mask_lower(2)
+            out0_copy(0)
+            interleave(on_scalar, "e0", E0_CUTS[1], E0_CUTS[2])
+
+            masks_and_sum(1)
+            turn(1)
+            warm_up_plain()
             turn_back(0)
-            add_upper(2)
             turn_gj(2)
-            quantize("e0", 0, 256)
-            turn_kept(2)
-            mask_upper(3)
-            turn_upper(2)
-            round_turned(2)
-            mask_lower(3)
-            warm_up_mx(0, 512)
-            add_upper(3)
+            round_turned(1)
+            interleave(on_scalar, "e0", E0_CUTS[2], E0_CUTS[3])
+            masks_and_sum(2)
+            turn(2)
+            warm_up_mx()
             turn_gj(3)
-            round_upper_scalar(0, 2, 3)
-            quantize_unit(1)
-            turn_kept(3)
-            mask_upper(4)
-            turn_upper(3)
-            round_turned(3)
-            mask_lower(4)
-            turn_back(1)
-            add_upper(4)
-            out0_product(1)
-            out0_copy(1, on_scalar)
-            quantize_unit(2)
-            out0_store(0, 2)
-            turn_gj(4)
-            quantize("e0", 256, 512)
-            turn_kept(4)
-            mask_upper(5)
-            turn_upper(4)
-            round_turned(4)
-            mask_lower(5)
-            turn_back(2)
-            add_upper(5)
-            out0_product(2)
-            out0_copy(2, on_scalar)
-            quantize_unit(3)
-            turn_gj(5)
-            round_upper_scalar(0, 3, 4)
-            quantize("dz0", 256, 384)
-            turn_kept(5)
-            mask_upper(6)
-            turn_upper(5)
-            round_turned(5)
-            mask_lower(6)
-            turn_back(3)
-            add_upper(6)
-            out0_product(3)
-            out0_copy(3, on_scalar)
-            quantize_unit(4)
-            out0_store(2, 2)
-            out1_product(0, 2)
-            mask_upper(7)
-            turn_gj(6)
-            mask_lower(7)
-            turn_kept(6)
-            add_upper(7)
-            turn_upper(6)
-            round_turned(6)
-            quantize_unit(5)
-            turn_back(4)
-            quantize("dz0", 384, 512)
-            out0_product(4)
-            out0_copy(4, on_scalar)
+            quantize("e0", 0, HALF)
+            round_turned(2)
+
+            for k in range(PACK - 1, UNITS):
+                masks_and_sum(k)
+                turn(k)
+                quantize_unit(k - LAG)
+                turn_back(k - LAG)
+                out0_product(k - LAG)
+                if k == PACK:
+                    quantize("e0", HALF, N)
+                for t in UPPER:
+                    if k == 2 * t + 1:
+                        quantize_tile(0, t)
+                        out1_product(0, t)
+                    if k == 2 * t - 1:
+                        round_upper(scaled_on_scalar, 0, t)
+                if k + 1 < UNITS:
+                    turn_gj(k + 1)
+                round_turned(k)
+                out0_copy(k - LAG)
+                if k % 2 == 1:
+                    out0_store(k - LAG - 1, 2)
+
             copy_back(on_vector, 0, 0)
-            turn_gj(7)
-            interleave(on_vector, "e1", 0, 256)
-            turn_kept(7)
-            quantize_unit(6)
-            turn_upper(7)
-            round_turned(7)
-            interleave(on_vector, "e1", 256, 512)
-            turn_back(5)
-            round_upper(1, 2, 3)
-            out0_product(5)
-            out0_copy(5, on_scalar)
-            quantize_unit(7)
-            out0_store(4, 2)
-            out1_product(0, 3)
+            interleave(on_vector, "e1", 0, HALF)
+            quantize_unit(UNITS - 2)
+            turn_back(UNITS - 2)
+            out0_product(UNITS - 2)
             copy_back(on_scalar, 0, 1)
-            quantize("e1", 0, 512)
-            turn_back(6)
-            quantize("dz1", 256, 384)
-            out0_product(6)
-            out0_copy(6, on_scalar)
-            round_upper(1, 3, 4)
-            out0_store(6, 1)
-            turn_back(7)
+            out0_copy(UNITS - 2)
+            out0_store(UNITS - 2, 1)
+            interleave(on_vector, "e1", HALF, N)
+            round_upper(scaled_on_vector, 1, 2)
+            turn_back(UNITS - 1)
+            quantize_unit(UNITS - 1)
+            out0_product(UNITS - 1)
             copy_back(on_scalar, 1, 0)
-            quantize("dz0", 0, 256)
-            out0_product(7)
-            out0_copy(7, on_scalar)
-            quantize("dz1", 384, 512)
-            out0_store(7, 1)
-            out1_product(1, 2)
+            out0_copy(UNITS - 1)
+            out0_store(UNITS - 1, 1)
             copy_back(on_scalar, 1, 1)
-            quantize("dz1", 0, 128)
+            quantize("e1", 0, N)
+            quantize_tile(1, 2)
+            out1_product(1, 2)
+            round_upper(scaled_on_vector, 1, 3)
+            quantize("dz0", 0, HALF)
+            quantize_tile(1, 3)
             out1_product(1, 3)
-            out1_copy(on_scalar, 3)
-            out1_copy(on_vector, 2)
-            out1_store(2, 1)
-            out1_store(3, 1)
+            quantize_tile(1, 0)
             out1_product(0, 0)
-            quantize("dz1", 128, 256)
             out1_product(1, 0)
-            out1_copy(on_vector, 0)
-            out1_store(0, 1)
+            out1_leave(on_vector, 2)
+            out1_leave(on_scalar, 3)
+            quantize_tile(1, LAST_TILE)
             last_product(0, 0)
             last_product(0, 1)
             last_product(1, 1)
-            last_copy(on_scalar, 1)
             last_product(1, 0)
+            out1_leave(on_vector, 0)
+            last_copy(on_scalar, 1)
             last_copy(on_vector, 0)
-            out1_store(1, 1)
+            out1_store(LAST_TILE)

@@ -25,14 +25,16 @@ GJ_WEIGHT = 20.0
 DZ_SCALE = 0.005
 LAG = 2
 
-EG1_ON_VECTOR = 320
-E0_CUTS = (0, 320, 384, N)
+
+SORTED = N - P
 
 TURN_BANKS = (0, 1)
 BACK_BANKS = (2, 3)
 OUT0_BANKS = (4, 5)
-OUT1_BANKS = {0: 2, 2: 6, 3: 7}
+SORT_BANK = 6
 WARM_BANK = 7
+OUT1_BANKS = {0: 0, 2: 7, 3: 4}
+LAST_BANKS = (1, 2)
 LAST_TILE = 1
 
 FLOPS = 2 * 2 * SAMPLES * N * N
@@ -60,6 +62,7 @@ def tile_bspncn_pb_v_kernel(tc, e_gen2, e_disc2, e_gen1, e_disc3, j2, v2, x2, Eg
             return psum.tile(shape, F32, name=f"bank{i}")
 
         ident = sb("ident", [P, P], F32)
+        ident_bf = sb("ident_bf", [P, P], BF16)
         ident_gj = sb("ident_gj", [P, P], BF16)
         v_pre_sb = [sb(f"v{k}", [P, N], F32) for k in range(UNITS)]
         grad_sb = [sb(f"grad{k}", [P, 2 * N], BF16) for k in range(UNITS)]
@@ -76,7 +79,7 @@ def tile_bspncn_pb_v_kernel(tc, e_gen2, e_disc2, e_gen1, e_disc3, j2, v2, x2, Eg
         dzt_scales = [sb(f"dzt_scales{k}", [P, P], U8) for k in range(UNITS)]
         out0_sb = [sb(f"out0_{g}", [P, PACK, N], F32) for g in range(2)]
         out1_sb = [sb(f"out1_{t}", [P, N], F32) for t in range(PACK)]
-        turned, back, out0_ps, out1_ps, last_ps = {}, {}, {}, {}, {}
+        turned, back, sorted_ps, out0_ps, out1_ps, last_ps = {}, {}, {}, {}, {}, {}
 
         def load_unit(k):
             nc.sync.dma_start(out=grad_sb[k][:], in_=grad_hbm[k // PACK][:, k % PACK, 0:2 * N])
@@ -121,9 +124,11 @@ def tile_bspncn_pb_v_kernel(tc, e_gen2, e_disc2, e_gen1, e_disc3, j2, v2, x2, Eg
             nc.vector.scalar_tensor_tensor(out=out, in0=by_slot(v_pre_sb[k][:], slots), scalar=THRESHOLD,
                                            in1=by_slot(grad_sb[k][:, N:2 * N], slots), op0=OP.is_lt, op1=OP.mult)
 
-        def masks_and_sum(k):
+        def masks(k):
             mask(k, UPPER, kept_upper[k][:])
             mask(k, LOWER, kept_lower[k][:].rearrange("p t q -> p q t"))
+
+        def upper_sum(k):
             nc.vector.scalar_tensor_tensor(out=s_upper[k // PACK][:, k % PACK, :].rearrange("p (t q) -> p t q", q=P),
                                            in0=by_slot(grad_sb[k][:, 0:N], UPPER).rearrange("p q t -> p t q"),
                                            scalar=GJ_WEIGHT, in1=kept_upper[k][:].rearrange("p q t -> p t q"),
@@ -197,116 +202,134 @@ def tile_bspncn_pb_v_kernel(tc, e_gen2, e_disc2, e_gen1, e_disc3, j2, v2, x2, Eg
 
         def last_product(g, h):
             if g == 0:
-                last_ps[h] = bank(TURN_BANKS[h], [P, HALF])
+                last_ps[h] = bank(LAST_BANKS[h], [P, HALF])
             times_e(g, LAST_TILE, slice(HALF * h, HALF * (h + 1)), last_ps[h][:])
 
         def last_copy(copy, h):
             copy(out1_sb[LAST_TILE][:, HALF * h:HALF * (h + 1)], last_ps[h][:])
 
+        def sort_on_tensor(name):
+            sorted_ps[name] = psum.tile([P, N], BF16, name=f"bank{SORT_BANK}")
+            nc.tensor.matmul(sorted_ps[name][:], lhsT=ident_bf[:],
+                             rhs=loaded[name][:, :, SORTED:N].rearrange("p j c -> p c j"), start=True, stop=True)
+
+        def copy_sorted(name):
+            on_scalar(grouped[name][:, SORTED:N, :].rearrange("p c j -> p (c j)"), sorted_ps[name][:])
+
         def warm_up_plain():
-            idle = bank(WARM_BANK, [P, N])
-            nc.tensor.matmul(idle[:], lhsT=ident_gj[:], rhs=loaded["Eg1"][:, 0, :], start=True, stop=True)
+            columns = P + P // 2
+            idle = bank(WARM_BANK, [P, columns])
+            nc.tensor.matmul(idle[:], lhsT=ident[:], rhs=v_pre_sb[0][:, 0:columns], start=True, stop=True)
 
         def warm_up_mx():
-            idle = bank(WARM_BANK, [P, N])
-            times_Eg1(0, idle[:])
+            idle = bank(WARM_BANK, [P, HALF])
+            nc.tensor.matmul_mx(out=idle[:], lhsT=dzt_codes[0][:].bitcast(E5M2), lhsT_scale=dzt_scales[0][:],
+                                rhs=codes["Eg1"][:, 0:HALF].bitcast(E4M3), rhs_scale=scales["Eg1"][:, 0:HALF],
+                                start=True, stop=True)
 
         make_identity(nc, ident[:])
+        make_identity(nc, ident_bf[:])
         with tc.manual_schedule():
             load_unit(0)
             load_operand("Eg1")
-            load_operand("e0")
             for k in range(1, UNITS):
                 load_unit(k)
+            load_operand("e0")
             load_operand("e1")
             nc.scalar.activation(out=ident_gj[:], in_=ident[:], func=COPY, scale=GJ_WEIGHT)
 
             turn_gj(0)
-            masks_and_sum(0)
+            masks(0)
+            upper_sum(0)
             turn(0)
-            interleave(on_scalar, "Eg1", EG1_ON_VECTOR, N)
-            interleave(on_vector, "Eg1", 0, EG1_ON_VECTOR)
-            round_turned(0)
-            interleave(on_scalar, "e0", E0_CUTS[0], E0_CUTS[1])
-            quantize("Eg1", 0, HALF)
-            quantize("Eg1", HALF, N)
-            quantize_unit(0)
+            sort_on_tensor("Eg1")
             turn_gj(1)
             warm_up_plain()
-            out0_product(0)
-            out0_copy(0)
-            interleave(on_scalar, "e0", E0_CUTS[1], E0_CUTS[2])
-
-            masks_and_sum(1)
+            interleave(on_vector, "Eg1", 0, HALF)
+            interleave(on_scalar, "Eg1", HALF, SORTED)
+            round_turned(0)
+            copy_sorted("Eg1")
+            quantize("Eg1", 0, HALF)
+            masks(1)
+            upper_sum(1)
             turn(1)
-            warm_up_plain()
-            turn_back(0)
             turn_gj(2)
             round_turned(1)
-            interleave(on_scalar, "e0", E0_CUTS[2], E0_CUTS[3])
-            masks_and_sum(2)
-            turn(2)
+            quantize_unit(0)
+            quantize("Eg1", HALF, N)
+            out0_product(0)
             warm_up_mx()
+            out0_copy(0)
+            masks(2)
+            upper_sum(2)
+            turn(2)
+            turn_back(0)
             turn_gj(3)
-            quantize("e0", 0, HALF)
+            warm_up_mx()
             round_turned(2)
 
             for k in range(PACK - 1, UNITS):
-                masks_and_sum(k)
+                masks(k)
+                upper_sum(k)
                 turn(k)
                 quantize_unit(k - LAG)
                 turn_back(k - LAG)
                 out0_product(k - LAG)
-                if k == PACK:
-                    quantize("e0", HALF, N)
-                for t in UPPER:
-                    if k == 2 * t + 1:
-                        quantize_tile(0, t)
-                        out1_product(0, t)
-                    if k == 2 * t - 1:
-                        round_upper(scaled_on_scalar, 0, t)
+                if k == PACK + 1:
+                    quantize("dz0", HALF, N)
                 if k + 1 < UNITS:
                     turn_gj(k + 1)
+                if k == UNITS - 2:
+                    warm_up_mx()
+                    copy_back(on_scalar, 0, LOWER[0])
+                if k == PACK - 1:
+                    round_upper(scaled_on_scalar, 0, UPPER[0])
                 round_turned(k)
+                if k == PACK - 1:
+                    round_upper(scaled_on_scalar, 0, UPPER[1])
                 out0_copy(k - LAG)
                 if k % 2 == 1:
                     out0_store(k - LAG - 1, 2)
 
-            copy_back(on_vector, 0, 0)
-            interleave(on_vector, "e1", 0, HALF)
+            interleave(on_vector, "e0", 0, N)
+            sort_on_tensor("e1")
+            copy_sorted("e1")
             quantize_unit(UNITS - 2)
             turn_back(UNITS - 2)
             out0_product(UNITS - 2)
-            copy_back(on_scalar, 0, 1)
+            turn_back(UNITS - 1)
             out0_copy(UNITS - 2)
             out0_store(UNITS - 2, 1)
-            interleave(on_vector, "e1", HALF, N)
-            round_upper(scaled_on_vector, 1, 2)
-            turn_back(UNITS - 1)
+            interleave(on_vector, "e1", 0, SORTED)
+            quantize("e0", 0, N)
+            out1_product(0, UPPER[0])
             quantize_unit(UNITS - 1)
             out0_product(UNITS - 1)
-            copy_back(on_scalar, 1, 0)
+            out1_product(0, UPPER[1])
+            copy_back(on_scalar, 0, LOWER[1])
+            copy_back(on_scalar, 1, LOWER[0])
             out0_copy(UNITS - 1)
             out0_store(UNITS - 1, 1)
-            copy_back(on_scalar, 1, 1)
+            copy_back(on_scalar, 1, LOWER[1])
+            round_upper(scaled_on_vector, 1, UPPER[0])
             quantize("e1", 0, N)
-            quantize_tile(1, 2)
-            out1_product(1, 2)
-            round_upper(scaled_on_vector, 1, 3)
+            quantize_tile(1, UPPER[0])
+            out1_product(1, UPPER[0])
+            round_upper(scaled_on_vector, 1, UPPER[1])
             quantize("dz0", 0, HALF)
-            quantize_tile(1, 3)
-            out1_product(1, 3)
-            quantize_tile(1, 0)
-            out1_product(0, 0)
-            out1_product(1, 0)
-            out1_leave(on_vector, 2)
-            out1_leave(on_scalar, 3)
-            quantize_tile(1, LAST_TILE)
+            out1_product(0, LOWER[0])
+            quantize_tile(1, UPPER[1])
+            out1_product(1, UPPER[1])
+            quantize_tile(1, LOWER[0])
+            out1_product(1, LOWER[0])
+            out1_leave(on_vector, UPPER[0])
+            out1_leave(on_scalar, UPPER[1])
             last_product(0, 0)
             last_product(0, 1)
+            quantize_tile(1, LAST_TILE)
             last_product(1, 1)
             last_product(1, 0)
-            out1_leave(on_vector, 0)
+            out1_leave(on_vector, LOWER[0])
             last_copy(on_scalar, 1)
             last_copy(on_vector, 0)
             out1_store(LAST_TILE)

@@ -273,7 +273,8 @@ def tile_bspncn_pb_v_kernel(tc, e_gen2, e_disc2, e_gen1, e_disc3, j2, v2, x2, Eg
                 upper_sum(k)
                 turn(k)
                 quantize_unit(k - LAG)
-                turn_back(k - LAG)
+                if k - LAG < PACK:
+                    turn_back(k - LAG)
                 out0_product(k - LAG)
                 if k == PACK + 1:
                     quantize("dz0", HALF, N)
@@ -281,7 +282,6 @@ def tile_bspncn_pb_v_kernel(tc, e_gen2, e_disc2, e_gen1, e_disc3, j2, v2, x2, Eg
                     turn_gj(k + 1)
                 if k == UNITS - 2:
                     warm_up_mx()
-                    copy_back(on_scalar, 0, LOWER[0])
                 if k == PACK - 1:
                     round_upper(scaled_on_scalar, 0, UPPER[0])
                 round_turned(k)
@@ -295,41 +295,42 @@ def tile_bspncn_pb_v_kernel(tc, e_gen2, e_disc2, e_gen1, e_disc3, j2, v2, x2, Eg
             sort_on_tensor("e1")
             copy_sorted("e1")
             quantize_unit(UNITS - 2)
-            turn_back(UNITS - 2)
             out0_product(UNITS - 2)
-            turn_back(UNITS - 1)
             out0_copy(UNITS - 2)
             out0_store(UNITS - 2, 1)
+            for k in range(PACK, UNITS):
+                turn_back(k)
             interleave(on_vector, "e1", 0, SORTED)
-            quantize("e0", 0, N)
-            out1_product(0, UPPER[0])
             quantize_unit(UNITS - 1)
             out0_product(UNITS - 1)
-            out1_product(0, UPPER[1])
-            copy_back(on_scalar, 0, LOWER[1])
+            copy_back(on_scalar, 0, LOWER[0])
             copy_back(on_scalar, 1, LOWER[0])
             out0_copy(UNITS - 1)
             out0_store(UNITS - 1, 1)
+            copy_back(on_scalar, 0, LOWER[1])
             copy_back(on_scalar, 1, LOWER[1])
             round_upper(scaled_on_vector, 1, UPPER[0])
-            quantize("e1", 0, N)
+            quantize("e0", 0, N)
+            out1_product(0, UPPER[0])
+            out1_product(0, UPPER[1])
             quantize_tile(1, UPPER[0])
+            quantize("e1", 0, N)
             out1_product(1, UPPER[0])
             round_upper(scaled_on_vector, 1, UPPER[1])
-            quantize("dz0", 0, HALF)
-            out1_product(0, LOWER[0])
+            for g in range(2):
+                quantize_tile(g, LOWER[0])
+                out1_product(g, LOWER[0])
             quantize_tile(1, UPPER[1])
             out1_product(1, UPPER[1])
-            quantize_tile(1, LOWER[0])
-            out1_product(1, LOWER[0])
             out1_leave(on_vector, UPPER[0])
-            out1_leave(on_scalar, UPPER[1])
+            out1_leave(on_scalar, LOWER[0])
+            quantize_tile(0, LAST_TILE)
             last_product(0, 0)
             last_product(0, 1)
             quantize_tile(1, LAST_TILE)
             last_product(1, 1)
             last_product(1, 0)
-            out1_leave(on_vector, LOWER[0])
+            out1_leave(on_vector, UPPER[1])
             last_copy(on_scalar, 1)
             last_copy(on_vector, 0)
             out1_store(LAST_TILE)

@@ -32,7 +32,6 @@ TURN_BANKS = (0, 1)
 BACK_BANKS = (2, 3)
 OUT0_BANKS = (4, 5)
 SORT_BANK = 6
-WARM_BANK = 7
 OUT1_BANKS = {0: 0, 2: 7, 3: 4}
 LAST_BANKS = (1, 2)
 LAST_TILE = 1
@@ -216,17 +215,6 @@ def tile_bspncn_pb_v_kernel(tc, e_gen2, e_disc2, e_gen1, e_disc3, j2, v2, x2, Eg
         def copy_sorted(name):
             on_scalar(grouped[name][:, SORTED:N, :].rearrange("p c j -> p (c j)"), sorted_ps[name][:])
 
-        def warm_up_plain():
-            columns = P + P // 2
-            idle = bank(WARM_BANK, [P, columns])
-            nc.tensor.matmul(idle[:], lhsT=ident[:], rhs=v_pre_sb[0][:, 0:columns], start=True, stop=True)
-
-        def warm_up_mx():
-            idle = bank(WARM_BANK, [P, HALF])
-            nc.tensor.matmul_mx(out=idle[:], lhsT=dzt_codes[0][:].bitcast(E5M2), lhsT_scale=dzt_scales[0][:],
-                                rhs=codes["Eg1"][:, 0:HALF].bitcast(E4M3), rhs_scale=scales["Eg1"][:, 0:HALF],
-                                start=True, stop=True)
-
         make_identity(nc, ident[:])
         make_identity(nc, ident_bf[:])
         with tc.manual_schedule():
@@ -244,7 +232,6 @@ def tile_bspncn_pb_v_kernel(tc, e_gen2, e_disc2, e_gen1, e_disc3, j2, v2, x2, Eg
             turn(0)
             sort_on_tensor("Eg1")
             turn_gj(1)
-            warm_up_plain()
             interleave(on_vector, "Eg1", 0, HALF)
             interleave(on_scalar, "Eg1", HALF, SORTED)
             round_turned(0)
@@ -258,14 +245,12 @@ def tile_bspncn_pb_v_kernel(tc, e_gen2, e_disc2, e_gen1, e_disc3, j2, v2, x2, Eg
             quantize_unit(0)
             quantize("Eg1", HALF, N)
             out0_product(0)
-            warm_up_mx()
             out0_copy(0)
             masks(2)
             upper_sum(2)
             turn(2)
             turn_back(0)
             turn_gj(3)
-            warm_up_mx()
             round_turned(2)
 
             for k in range(PACK - 1, UNITS):
@@ -280,8 +265,6 @@ def tile_bspncn_pb_v_kernel(tc, e_gen2, e_disc2, e_gen1, e_disc3, j2, v2, x2, Eg
                     quantize("dz0", HALF, N)
                 if k + 1 < UNITS:
                     turn_gj(k + 1)
-                if k == UNITS - 2:
-                    warm_up_mx()
                 if k == PACK - 1:
                     round_upper(scaled_on_scalar, 0, UPPER[0])
                 round_turned(k)

from contextlib import ExitStack

import concourse.mybir as mybir
from concourse.masks import make_identity

F32 = mybir.dt.float32
BF16 = mybir.dt.bfloat16
U32 = mybir.dt.uint32
U8 = mybir.dt.uint8
E4M3 = mybir.dt.float8_e4m3fn_x4
E5M2 = mybir.dt.float8_e5m2_x4
OP = mybir.AluOpType
COPY = mybir.ActivationFunctionType.Copy

P = 128
PACK = 4
N = 512
HALF = N // 2
SAMPLES = 1024
UNITS = SAMPLES // P
LOWER = (0, 1)
UPPER = (2, 3)
THRESHOLD = 0.4
GJ_WEIGHT = 20.0
DZ_SCALE = 0.005
LAG = 2


SORTED = N - P

TURN_BANKS = (0, 1)
BACK_BANKS = (2, 3)
OUT0_BANKS = (4, 5)
SORT_BANK = 6
OUT1_BANKS = {0: 0, 2: 7, 3: 4}
LAST_BANKS = (1, 2)
LAST_TILE = 1

FLOPS = 2 * 2 * SAMPLES * N * N
BYTES = SAMPLES * N * (4 + 2 + 2 + 2) + N * N * 2 + SAMPLES * N * 4 + N * N * 4


def tile_bspncn_pb_v_kernel(tc, e_gen2, e_disc2, e_gen1, e_disc3, j2, v2, x2, Eg1, Ed2, v_pre, grad_out, out_0, out_1):
    nc = tc.nc
    by_sample = "(g p j) w -> g p j w"
    v_hbm = v_pre.rearrange(by_sample, p=P, j=PACK)
    grad_hbm = grad_out.rearrange(by_sample, p=P, j=PACK)
    e_hbm = e_gen1.rearrange(by_sample, p=P, j=PACK)
    out0_hbm = out_0.rearrange(by_sample, p=P, j=PACK)
    out1_hbm = out_1.rearrange("(q t) w -> q t w", t=PACK)
    operand_hbm = {"Eg1": Eg1.rearrange("(q t) w -> q t w", t=PACK), "e0": e_hbm[0], "e1": e_hbm[1]}

    with ExitStack() as ctx:
        sbuf = ctx.enter_context(tc.tile_pool(name="sbuf", bufs=1))
        psum = ctx.enter_context(tc.psum_pool(name="psum", bufs=1))

        def sb(name, shape, dtype):
            return sbuf.tile(shape, dtype, name=name, align_bytes=64)

        def bank(i, shape):
            return psum.tile(shape, F32, name=f"bank{i}")

        ident = sb("ident", [P, P], F32)
        ident_bf = sb("ident_bf", [P, P], BF16)
        ident_gj = sb("ident_gj", [P, P], BF16)
        v_pre_sb = [sb(f"v{k}", [P, N], F32) for k in range(UNITS)]
        grad_sb = [sb(f"grad{k}", [P, 2 * N], BF16) for k in range(UNITS)]
        kept_lower = [sb(f"kept_lower{k}", [P, 2, P], F32) for k in range(UNITS)]
        kept_upper = [sb(f"kept_upper{k}", [P, P, 2], BF16) for k in range(UNITS)]
        s_upper = [sb(f"s_upper{g}", [P, PACK, HALF], F32) for g in range(2)]
        loaded = {name: sb(f"loaded_{name}", [P, PACK, N], BF16) for name in operand_hbm}
        wide = ("Eg1", "e0", "e1", "dz0", "dz1")
        grouped = {name: sb(f"grouped_{name}", [P, N, PACK], BF16) for name in wide}
        codes = {name: sb(f"codes_{name}", [P, N], U32) for name in wide}
        scales = {name: sb(f"scales_{name}", [P, N], U8) for name in wide}
        dzt = [sb(f"dzt{k}", [P, P * PACK], BF16) for k in range(UNITS)]
        dzt_codes = [sb(f"dzt_codes{k}", [P, P], U32) for k in range(UNITS)]
        dzt_scales = [sb(f"dzt_scales{k}", [P, P], U8) for k in range(UNITS)]
        out0_sb = [sb(f"out0_{g}", [P, PACK, N], F32) for g in range(2)]
        out1_sb = [sb(f"out1_{t}", [P, N], F32) for t in range(PACK)]
        turned, back, sorted_ps, out0_ps, out1_ps, last_ps = {}, {}, {}, {}, {}, {}

        def load_unit(k):
            nc.sync.dma_start(out=grad_sb[k][:], in_=grad_hbm[k // PACK][:, k % PACK, 0:2 * N])
            nc.sync.dma_start(out=v_pre_sb[k][:], in_=v_hbm[k // PACK][:, k % PACK, :])

        def load_operand(name):
            nc.sync.dma_start(out=loaded[name][:], in_=operand_hbm[name])

        def on_vector(out, in_):
            nc.vector.tensor_copy(out=out, in_=in_)

        def on_scalar(out, in_):
            nc.scalar.copy(out=out, in_=in_)

        def scaled_on_vector(out, in_):
            nc.vector.tensor_scalar(out=out, in0=in_, scalar1=DZ_SCALE, scalar2=None, op0=OP.mult)

        def scaled_on_scalar(out, in_):
            nc.scalar.activation(out=out, in_=in_, func=COPY, scale=DZ_SCALE)

        def slots_first(ap):
            return ap.rearrange("p j (c i) -> p c j i", i=4)

        def slots_last(ap):
            return ap.rearrange("p (c i) j -> p c j i", i=4)

        def interleave(copy, name, c0, c1):
            copy(slots_last(grouped[name][:, c0:c1, :]), slots_first(loaded[name][:, :, c0:c1]))

        def quantize(name, c0, c1):
            fmt = E5M2 if name.startswith("dz") else E4M3
            nc.vector.quantize_mx(out=codes[name][:, c0:c1].bitcast(fmt), scales=scales[name][:, c0:c1],
                                  in_=grouped[name][:, c0:c1, :].rearrange("p c j -> p (c j)"))

        def quantize_tile(g, t):
            quantize(f"dz{g}", P * t, P * (t + 1))

        def by_slot(ap, slots):
            return ap.rearrange("p (q t) -> p q t", t=PACK)[:, :, slots[0]:slots[1] + 1]

        def mask(k, slots, out):
            nc.vector.scalar_tensor_tensor(out=out, in0=by_slot(v_pre_sb[k][:], slots), scalar=THRESHOLD,
                                           in1=by_slot(grad_sb[k][:, N:2 * N], slots), op0=OP.is_lt, op1=OP.mult)

        def masks(k):
            mask(k, UPPER, kept_upper[k][:])
            mask(k, LOWER, kept_lower[k][:].rearrange("p t q -> p q t"))

        def upper_sum(k):
            nc.vector.scalar_tensor_tensor(out=s_upper[k // PACK][:, k % PACK, :].rearrange("p (t q) -> p t q", q=P),
                                           in0=by_slot(grad_sb[k][:, 0:N], UPPER).rearrange("p q t -> p t q"),
                                           scalar=GJ_WEIGHT, in1=kept_upper[k][:].rearrange("p q t -> p t q"),
                                           op0=OP.mult, op1=OP.add)

        def turn_gj(k):
            turned[k] = bank(TURN_BANKS[k % 2], [P, PACK, P])
            for t in LOWER:
                nc.tensor.matmul(turned[k][:, t, :], lhsT=grad_sb[k][:, t:N:PACK], rhs=ident_gj[:],
                                 start=(t == LOWER[0]), stop=False)

        def turn(k):
            for t in LOWER:
                nc.tensor.matmul(turned[k][:, t, :], lhsT=kept_lower[k][:, t, :], rhs=ident[:], is_transpose=True,
                                 start=False, stop=(t == LOWER[1]))
            for i, t in enumerate(UPPER):
                nc.tensor.transpose(turned[k][:, t, :], s_upper[k // PACK][:, k % PACK, P * i:P * (i + 1)], ident[:])

        def round_turned(k):
            scaled_on_scalar(dzt[k][:].rearrange("q (p t) -> q p t", t=PACK), turned[k][:].rearrange("q t p -> q p t"))

        def round_upper(scaled_copy, g, t):
            i = t - UPPER[0]
            scaled_copy(slots_last(grouped[f"dz{g}"][:, P * t:P * (t + 1), :]), slots_first(s_upper[g][:, :, P * i:P * (i + 1)]))

        def turn_back(k):
            g = k // PACK
            if k % PACK == 0:
                back[g] = bank(BACK_BANKS[g], [P, PACK, P])
            nc.tensor.transpose(back[g][:, k % PACK, :], dzt[k][:].bitcast(F32)[:, 0:2 * P:2], ident[:])

        def copy_back(copy, g, t):
            halves = back[g][:].rearrange("p j q -> p (j q)").bitcast(BF16).rearrange("p (j q e) -> p e q j", j=PACK, e=2)
            copy(grouped[f"dz{g}"][:, P * t:P * (t + 1), :], halves[:, t, :, :])

        def quantize_unit(k):
            nc.vector.quantize_mx(out=dzt_codes[k][:].bitcast(E5M2), scales=dzt_scales[k][:], in_=dzt[k][:])

        def times_Eg1(k, out):
            nc.tensor.matmul_mx(out=out, lhsT=dzt_codes[k][:].bitcast(E5M2), lhsT_scale=dzt_scales[k][:],
                                rhs=codes["Eg1"][:].bitcast(E4M3), rhs_scale=scales["Eg1"][:], start=True, stop=True)

        def out0_product(k):
            out0_ps[k] = bank(OUT0_BANKS[k % 2], [P, N])
            times_Eg1(k, out0_ps[k][:])

        def out0_copy(k):
            on_scalar(out0_sb[k // PACK][:, k % PACK, :], out0_ps[k][:])

        def out0_store(k, n):
            j = slice(k % PACK, k % PACK + n)
            nc.sync.dma_start(out=out0_hbm[k // PACK][:, j, :], in_=out0_sb[k // PACK][:, j, :])

        def times_e(g, t, n, out):
            c = slice(P * t, P * (t + 1))
            nc.tensor.matmul_mx(out=out, lhsT=codes[f"dz{g}"][:, c].bitcast(E5M2), lhsT_scale=scales[f"dz{g}"][:, c],
                                rhs=codes[f"e{g}"][:, n].bitcast(E4M3), rhs_scale=scales[f"e{g}"][:, n],
                                start=(g == 0), stop=(g == 1))

        def out1_product(g, t):
            if g == 0:
                out1_ps[t] = bank(OUT1_BANKS[t], [P, N])
            times_e(g, t, slice(0, N), out1_ps[t][:])

        def out1_store(t):
            nc.sync.dma_start(out=out1_hbm[:, t, :], in_=out1_sb[t][:])

        def out1_leave(copy, t):
            copy(out1_sb[t][:], out1_ps[t][:])
            out1_store(t)

        def last_product(g, h):
            if g == 0:
                last_ps[h] = bank(LAST_BANKS[h], [P, HALF])
            times_e(g, LAST_TILE, slice(HALF * h, HALF * (h + 1)), last_ps[h][:])

        def last_copy(copy, h):
            copy(out1_sb[LAST_TILE][:, HALF * h:HALF * (h + 1)], last_ps[h][:])

        def sort_on_tensor(name):
            sorted_ps[name] = psum.tile([P, N], BF16, name=f"bank{SORT_BANK}")
            nc.tensor.matmul(sorted_ps[name][:], lhsT=ident_bf[:],
                             rhs=loaded[name][:, :, SORTED:N].rearrange("p j c -> p c j"), start=True, stop=True)

        def copy_sorted(name):
            on_scalar(grouped[name][:, SORTED:N, :].rearrange("p c j -> p (c j)"), sorted_ps[name][:])

        make_identity(nc, ident[:])
        make_identity(nc, ident_bf[:])
        with tc.manual_schedule():
            load_unit(0)
            load_operand("Eg1")
            for k in range(1, UNITS):
                load_unit(k)
            load_operand("e0")
            load_operand("e1")
            nc.scalar.activation(out=ident_gj[:], in_=ident[:], func=COPY, scale=GJ_WEIGHT)

            turn_gj(0)
            masks(0)
            upper_sum(0)
            turn(0)
            sort_on_tensor("Eg1")
            turn_gj(1)
            interleave(on_vector, "Eg1", 0, HALF)
            interleave(on_scalar, "Eg1", HALF, SORTED)
            round_turned(0)
            copy_sorted("Eg1")
            quantize("Eg1", 0, HALF)
            masks(1)
            upper_sum(1)
            turn(1)
            turn_gj(2)
            round_turned(1)
            quantize_unit(0)
            quantize("Eg1", HALF, N)
            out0_product(0)
            out0_copy(0)
            masks(2)
            upper_sum(2)
            turn(2)
            turn_back(0)
            turn_gj(3)
            round_turned(2)

            for k in range(PACK - 1, UNITS):
                masks(k)
                upper_sum(k)
                turn(k)
                quantize_unit(k - LAG)
                if k - LAG < PACK:
                    turn_back(k - LAG)
                out0_product(k - LAG)
                if k == PACK + 1:
                    quantize("dz0", HALF, N)
                if k + 1 < UNITS:
                    turn_gj(k + 1)
                if k == PACK - 1:
                    round_upper(scaled_on_scalar, 0, UPPER[0])
                round_turned(k)
                if k == PACK - 1:
                    round_upper(scaled_on_scalar, 0, UPPER[1])
                out0_copy(k - LAG)
                if k % 2 == 1:
                    out0_store(k - LAG - 1, 2)

            interleave(on_vector, "e0", 0, N)
            sort_on_tensor("e1")
            copy_sorted("e1")
            quantize_unit(UNITS - 2)
            out0_product(UNITS - 2)
            out0_copy(UNITS - 2)
            out0_store(UNITS - 2, 1)
            for k in range(PACK, UNITS):
                turn_back(k)
            interleave(on_vector, "e1", 0, SORTED)
            quantize_unit(UNITS - 1)
            out0_product(UNITS - 1)
            copy_back(on_scalar, 0, LOWER[0])
            copy_back(on_scalar, 1, LOWER[0])
            out0_copy(UNITS - 1)
            out0_store(UNITS - 1, 1)
            copy_back(on_scalar, 0, LOWER[1])
            copy_back(on_scalar, 1, LOWER[1])
            round_upper(scaled_on_vector, 1, UPPER[0])
            quantize("e0", 0, N)
            out1_product(0, UPPER[0])
            out1_product(0, UPPER[1])
            quantize_tile(1, UPPER[0])
            quantize("e1", 0, N)
            out1_product(1, UPPER[0])
            round_upper(scaled_on_vector, 1, UPPER[1])
            for g in range(2):
                quantize_tile(g, LOWER[0])
                out1_product(g, LOWER[0])
            quantize_tile(1, UPPER[1])
            out1_product(1, UPPER[1])
            out1_leave(on_vector, UPPER[0])
            out1_leave(on_scalar, LOWER[0])
            quantize_tile(0, LAST_TILE)
            last_product(0, 0)
            last_product(0, 1)
            quantize_tile(1, LAST_TILE)
            last_product(1, 1)
            last_product(1, 0)
            out1_leave(on_vector, UPPER[1])
            last_copy(on_scalar, 1)
            last_copy(on_vector, 0)
            out1_store(LAST_TILE)
